import numpy as np
import ml_dtypes


def mxq(x, axis, fmt="e4m3"):
    dtype, down = {"e4m3": (ml_dtypes.float8_e4m3fn, 7), "e5m2": (ml_dtypes.float8_e5m2, 14)}[fmt]
    v = np.moveaxis(np.asarray(x, np.float32).astype(ml_dtypes.bfloat16).astype(np.float64), axis, -1)
    blocks = v.reshape(v.shape[:-1] + (-1, 32))
    amax = np.abs(blocks).max(-1, keepdims=True)
    byte = np.maximum(np.where(amax > 0, np.frexp(amax)[1] - 1 + 127, 0) - down, 1)
    scale = np.exp2(byte - 127.0)
    codes = (blocks / scale).astype(np.float32).astype(dtype).astype(np.float64)
    return np.moveaxis((codes * scale).reshape(v.shape), -1, axis)


WIDE = False


def mx_kscale(k):
    if not WIDE:
        return np.ones(k)
    levels = np.array([18, -18])
    if k % 512:
        return np.exp2(np.random.permutation(np.resize(levels, k // 32))).repeat(32)
    a = np.empty((k // 512, 16))
    for p in range(k // 512):
        a[p, :8] = np.random.permutation(np.resize(levels, 8))
        for g in range(8):
            far = levels[np.abs(levels - a[p, g]) >= 10]
            a[p, g + 8] = far[np.random.randint(len(far))]
    return np.exp2(a.ravel()).repeat(32)


BF16 = ml_dtypes.bfloat16


def bf(x):
    return np.asarray(x, np.float32).astype(BF16)


def f64(x):
    return np.asarray(x).astype(np.float64)


B, N, C = 128, 4, 1024
T = B * N
NEG_SLOPE = 0.2


def leaky(v):
    return np.where(v >= 0, v, NEG_SLOPE * v)


def leaky_grad(v):
    return np.where(v >= 0, 1.0, NEG_SLOPE)


def setup_inputs():
    s = mx_kscale(T).reshape(B, N, 1)
    u = mx_kscale(C)
    v = mx_kscale(C)
    W1_0 = bf((np.random.standard_normal((2, C, C)) * 0.7 / np.sqrt(C)).reshape(2 * C, C))
    F0 = bf(np.random.standard_normal((B, N, C)))
    b1 = bf(np.random.standard_normal(C) * 0.2)
    W2_0 = bf(np.random.standard_normal((C, C)) / np.sqrt(C))
    b2 = bf(np.random.standard_normal(C) * 0.2)
    g = bf(np.random.standard_normal((B, N, C)) * np.exp2(np.random.randint(-6, 1, (B, N, 1))) / s * u)
    A = f64(F0) @ f64(W1_0)[:C]
    Bp = f64(F0) @ f64(W1_0)[C:]
    z1 = A[:, :, None, :] + Bp[:, None, :, :] + f64(b1)
    z2 = leaky(z1) @ f64(W2_0) + f64(b2)
    return {"F": bf(f64(F0) * s), "W1": bf(f64(W1_0) / v), "b1": b1, "W2": bf(f64(W2_0) * v[:, None] / u), "b2": b2,
            "z1": np.asarray(z1, np.float32), "z2": np.asarray(z2, np.float32), "grad_out": g}


def reference(F, W1, b1, W2, b2, z1, z2, grad_out):
    W1f = f64(W1)
    dz2 = f64(grad_out)[:, :, None, :] * leaky_grad(f64(z2))
    dh = mxq(dz2.reshape(B * N * N, C), 1, "e5m2") @ mxq(f64(W2), 1, "e4m3").T
    dp = dh.reshape(B, N, N, C) * leaky_grad(f64(z1))
    dA = dp.sum(2).reshape(T, C)
    dB = dp.sum(1).reshape(T, C)
    dz1 = np.concatenate([dA, dB], axis=1)
    Wc = np.concatenate([W1f[:C], W1f[C:]], axis=1)
    dF = mxq(dz1, 1, "e5m2") @ mxq(Wc, 1, "e4m3").T
    dWc = mxq(f64(F).reshape(T, C), 0, "e4m3").T @ mxq(dz1, 0, "e5m2")
    dW1 = np.concatenate([dWc[:, :C], dWc[:, C:]], axis=0)
    return dF.reshape(B, N, C), dW1

@@ -1,0 +1,472 @@
+from contextlib import ExitStack
+
+import concourse.mybir as mybir
+from concourse.masks import make_identity
+
+F32 = mybir.dt.float32
+BF16 = mybir.dt.bfloat16
+U32 = mybir.dt.uint32
+U8 = mybir.dt.uint8
+E4 = mybir.dt.float8_e4m3fn_x4
+E5 = mybir.dt.float8_e5m2_x4
+ALU = mybir.AluOpType
+ACT = mybir.ActivationFunctionType
+
+P = 128
+NODES = 4
+C = 1024
+KP = 512
+SLOPE = 0.2
+TINY = 2.0 ** -126
+FLOPS = 2 * 2048 * C * C + 2 * 2 * 512 * 2048 * C
+BYTES = 2 * (512 * C * 2 + 3 * C * C) + 4 * (2 * 2048 * C + 512 * C + 2048 * C)
+
+RAW_BUFS = 17
+JOBS = (0, 4, 2, 0, 2, 2, 2, 2, 6, 6)
+OUTS = (2, 2, 2, 2, 3, 2, 0)
+OUT_V = 1
+M1_V = (0, 3, 5)
+M2_V = (1,)
+ADD_G = True
+F_AT = 2
+F_ENG = "G"
+F_LEAD = 0.95
+Z1_LEAD = 0.0
+W_LEAD = 0.5
+TB_SPLIT = 160
+EV_V = 2
+TB_ENG = "V"
+T10 = "SSSS"
+S_ONLY = 6
+WST = 5
+
+
+def tile_nonlocalmp_pa_v_kernel(tc, F, W1, b1, W2, b2, z1, z2, grad_out, out_0, out_1):
+    nc = tc.nc
+    with ExitStack() as ctx:
+        keep = ctx.enter_context(tc.tile_pool(name="keep", bufs=1))
+        work = ctx.enter_context(tc.tile_pool(name="work", bufs=2))
+        psum = ctx.enter_context(tc.psum_pool(name="psum", bufs=1))
+        ctx.enter_context(tc.manual_schedule())
+
+        ident32 = keep.tile([P, P], F32, name="ident32")
+        ident16 = keep.tile([P, P], BF16, name="ident16")
+        make_identity(nc, ident32[:])
+        make_identity(nc, ident16[:])
+
+        def mx_store(name, cols):
+            codes = keep.tile([P, cols], U32, name=name + "_codes", align_bytes=64)
+            scales = keep.tile([P, cols], U8, name=name + "_scales", align_bytes=64)
+            return codes, scales
+
+        dz2_q = [mx_store("dz2q%d" % s, KP) for s in range(8)]
+        w2_q = {(h, g): mx_store("w2q%d%d" % (h, g), KP) for h in range(2) for g in range(2)}
+        w1_q = {(a, x, h): mx_store("w1q%d%d%d" % (a, x, h), KP) for a in range(2) for x in range(2) for h in range(2)}
+        f_q = [mx_store("fq%d" % x, KP) for x in range(2)]
+        feat_q = {(a, h): mx_store("featq%d%d" % (a, h), KP) for a in range(2) for h in range(2)}
+        tok_q = {(a, h): mx_store("tokq%d%d" % (a, h), KP) for a in range(2) for h in range(2)}
+        g_t = {(g, q): keep.tile([P, 2, P, 4], BF16, name="gt%d%d" % (g, q)) for g in range(2) for q in range(2)}
+
+        def quantize(store, c0, fmt, src):
+            n = src.shape[1] // 4
+            nc.vector.quantize_mx(out=store[0][:, c0:c0 + n].bitcast(fmt), scales=store[1][:, c0:c0 + n], in_=src)
+
+        def mx(bank, lhs, l0, lfmt, rhs, rfmt, start, stop):
+            nc.tensor.matmul_mx(out=bank[:], lhsT=lhs[0][:, l0:l0 + P].bitcast(lfmt), lhsT_scale=lhs[1][:, l0:l0 + P],
+                                rhs=rhs[0][:].bitcast(rfmt), rhs_scale=rhs[1][:], start=start, stop=stop)
+
+        def copy_on(engine, out, in_):
+            if engine == "S":
+                nc.scalar.copy(out=out, in_=in_)
+            else:
+                nc.vector.tensor_copy(out=out, in_=in_)
+
+        def rows4(w, x, q):
+            return w[KP * x:KP * (x + 1), :].rearrange("(m r) k -> m r k", r=4)[:, 2 * q:2 * q + 2, :]
+
+        def source(key):
+            kind = key[0]
+            if kind == "z2":
+                s, g = key[1:]
+                return z2[:, s // 2, 2 * (s % 2):2 * (s % 2) + 2, KP * g:KP * (g + 1)]
+            if kind == "z1":
+                h, s = divmod(key[1], 8)
+                return z1[:, s // 2, 2 * (s % 2):2 * (s % 2) + 2, KP * h:KP * (h + 1)]
+            if kind == "g":
+                return grad_out[:, 2 * key[1]:2 * key[1] + 2, :]
+            if kind == "w2":
+                return rows4(W2, key[1], key[2])
+            if kind == "w1":
+                return rows4(W1, key[1], key[2])
+            return F[:, :, KP * key[1]:KP * (key[1] + 1)]
+
+        turn_units = [("w2", 0, 0), ("w2", 0, 1), ("g", 1), ("w2", 1, 0), ("w2", 1, 1)] + [("w1", x, q) for x in range(4) for q in range(2)]
+        jobs = [(u, g) for u in turn_units for g in range(2)]
+        slots = [t for t, n in enumerate(JOBS) for k in range(n)]
+        job_tick = dict(zip(jobs, slots))
+        need = [(-3, ("z2", 0, 0)), (-2.5, ("g", 0)), (-2, ("z2", 0, 1))]
+        need.extend([(s - 1.2 + 0.1 * g, ("z2", s, g)) for s in range(1, 8) for g in range(2)])
+        need.extend([(u + 0.9 - Z1_LEAD, ("z1", u)) for u in range(16)])
+        need.extend([(job_tick[(u, 0)] - W_LEAD, u) for u in turn_units])
+        need.extend([(F_AT - F_LEAD + x, ("f", x)) for x in range(2)])
+        order = [key for rank, key in sorted(need)]
+        raw = {}
+        done = set()
+
+        def pump():
+            while len(raw) < len(order) and (len(raw) < RAW_BUFS or order[len(raw) - RAW_BUFS] in done):
+                key = order[len(raw)]
+                src = source(key)
+                tile = work.tile(list(src.shape), src.dtype, name="raw", bufs=RAW_BUFS)
+                nc.sync.dma_start(out=tile[:], in_=src)
+                raw[key] = tile
+
+        def release(key):
+            done.add(key)
+            pump()
+
+        def turn_pe(unit, g, tag="misc"):
+            words = raw[unit][:].rearrange("p r k -> p (r k)").bitcast(F32)
+            bank = psum.tile([P, 2, 2, P], F32, name=tag, bufs=2)
+            for r in range(2):
+                for u in range(2):
+                    w0 = KP * r + 256 * g
+                    nc.tensor.transpose(bank[:, r, u, :], words[:, w0 + u:w0 + 256:2], ident32[:])
+            if g == 1:
+                release(unit)
+            return bank
+
+        def turn_out(unit, g, bank, engine):
+            if unit[0] == "g":
+                dst = g_t[(g, unit[1])]
+            else:
+                dst = work.tile([P, 2, P, 4], BF16, name="wstage", bufs=WST, align_bytes=64)
+            words = dst[:].rearrange("p r m t -> p (r m t)").bitcast(F32).rearrange("p (r m u) -> p r m u", r=2, u=2)
+            copy_on(engine, words, bank[:].rearrange("p r u m -> p r m u"))
+            return dst
+
+        def turn_quant(unit, g, stage):
+            if unit[0] == "w2":
+                store = w2_q[(unit[1], g)]
+            else:
+                store = w1_q[(unit[1] // 2, unit[1] % 2, g)]
+            quantize(store, 256 * unit[2], E4, stage[:].rearrange("p r m t -> p (r m t)"))
+
+        def sign_of(engine, out, in_):
+            if engine == "S":
+                nc.scalar.activation(out=out, in_=in_, func=ACT.Sign, bias=TINY)
+            else:
+                nc.vector.tensor_scalar(out=out, in0=in_, scalar1=0.0, scalar2=None, op0=ALU.is_ge)
+
+        sign2 = {}
+        sign2_t = {}
+        dz2_t = {}
+        sign1 = {}
+        dh = {}
+        dp = {}
+        acc = {}
+        db = {}
+        feat = {}
+        tok = {}
+
+        def mask2(s, g, engine):
+            tile = work.tile([P, 4, P, 2], BF16, name="sign2", bufs=3)
+            sign_of(engine, tile[:].rearrange("b t p j -> b p t j"), raw[("z2", s, g)][:].rearrange("b j (p t) -> b p t j", t=4))
+            sign2[(s, g)] = tile
+            release(("z2", s, g))
+
+        def turn2(s, g):
+            words = sign2[(s, g)][:].rearrange("b t p j -> b (t p j)").bitcast(F32)
+            bank = psum.tile([P, 4, P], F32, name="tz", bufs=2)
+            for t in range(4):
+                nc.tensor.transpose(bank[:, t, :], words[:, P * t:P * (t + 1)], ident32[:])
+            sign2_t[(s, g)] = bank
+
+        def make_dz2(s, g, j):
+            if (g, j) == (0, 0):
+                dz2_t[s] = work.tile([P, 2, 2, P, 4], BF16, name="dz2t", bufs=2, align_bytes=64)
+            signs = sign2_t[(s, g)][:].rearrange("p t b -> p (t b)").bitcast(BF16).rearrange("p (t b j) -> p j b t", t=4, j=2)
+            i = s // 2
+            nc.vector.scalar_tensor_tensor(out=dz2_t[s][:, j, g], in0=signs[:, j], scalar=SLOPE, in1=g_t[(g, i // 2)][:, i % 2],
+                                           op0=ALU.max, op1=ALU.mult)
+
+        def quant_dz2(s):
+            quantize(dz2_q[s], 0, E5, dz2_t[s][:].rearrange("p j g b t -> p (j g b t)"))
+
+        def make_dh(u, j):
+            h, s = divmod(u, 8)
+            bank = psum.tile([P, KP], F32, name="dh", bufs=3)
+            for g in range(2):
+                mx(bank, dz2_q[s], P * (2 * j + g), E5, w2_q[(h, g)], E4, g == 0, g == 1)
+            dh[(u, j)] = bank
+
+        def mask1(u, engine):
+            tile = work.tile([P, 2, 4, P], F32, name="sign1", bufs=3)
+            sign_of(engine, tile[:].rearrange("b j t p -> b j p t"), raw[("z1", u)][:].rearrange("b j (p t) -> b j p t", t=4))
+            sign1[u] = tile
+            release(("z1", u))
+
+        def make_dp(u, j):
+            h, s = divmod(u, 8)
+            i, node = s // 2, 2 * (s % 2) + j
+            tile = work.tile([P, KP], F32, name="dp", bufs=9)
+            nc.vector.scalar_tensor_tensor(out=tile[:], in0=sign1[u][:, j].rearrange("b t p -> b (t p)"), scalar=SLOPE, in1=dh[(u, j)][:],
+                                           op0=ALU.max, op1=ALU.mult)
+            dp[(h, i, node)] = tile
+            if u < 15:
+                add_db(u, j, nc.gpsimd)
+
+        def add_db(u, j, adder):
+            h, s = divmod(u, 8)
+            i, node = s // 2, 2 * (s % 2) + j
+            tile = dp[(h, i, node)]
+            if i == 1:
+                acc[node] = work.tile([P, KP], F32, name="acc", bufs=4)
+                adder.tensor_tensor(out=acc[node][:], in0=dp[(h, 0, node)][:], in1=tile[:], op=ALU.add)
+            elif i == 2:
+                adder.tensor_tensor(out=acc[node][:], in0=acc[node][:], in1=tile[:], op=ALU.add)
+            elif i == 3:
+                if node == 0:
+                    db[h] = work.tile([P, NODES, KP], BF16, name="db", bufs=1)
+                adder.tensor_tensor(out=db[h][:, node], in0=acc[node][:], in1=tile[:], op=ALU.add)
+
+        def sum_da_pe(h, i):
+            bank = psum.tile([P, 4, P], F32, name="da", bufs=1)
+            for t in range(4):
+                for node in range(NODES):
+                    nc.tensor.matmul(bank[:, t, :], lhsT=dp[(h, i, node)][:, P * t:P * (t + 1)], rhs=ident32[:],
+                                     start=node == 0, stop=node == NODES - 1, is_transpose=True)
+            return bank
+
+        def sum_da_node(h, i, node, bank):
+            for t in range(4):
+                nc.tensor.matmul(bank[:, t, :], lhsT=dp[(h, i, node)][:, P * t:P * (t + 1)], rhs=ident32[:],
+                                 start=(node, t) == (0, 0), stop=(node, t) == (NODES - 1, 3), is_transpose=True)
+
+        def sum_da_out(h, i, bank, engine):
+            if i == 0:
+                feat[(0, h)] = work.tile([P, NODES, P, 4], BF16, name="feat", bufs=3, align_bytes=64)
+            copy_on(engine, feat[(0, h)][:, i], bank[:].rearrange("p t b -> p b t"))
+
+        def quant_feat(a, h):
+            quantize(feat_q[(a, h)], 0, E5, feat[(a, h)][:].rearrange("p n b t -> p (n b t)"))
+
+        def back_a_pe(h, u, tag):
+            words = feat[(0, h)][:].rearrange("p n b t -> p (n b t)").bitcast(F32)
+            bank = psum.tile([P, NODES, P], F32, name=tag, bufs=2)
+            for i in range(NODES):
+                nc.tensor.transpose(bank[:, i, :], words[:, 256 * i + u:256 * (i + 1):2], ident32[:])
+            return bank
+
+        def back_a_out(h, u, bank, engine):
+            if u == 0:
+                tok[(0, h)] = work.tile([P, KP, NODES], BF16, name="tok", bufs=2, align_bytes=64)
+            values = bank[:].rearrange("b n p -> b (n p)").bitcast(BF16).rearrange("b (n c) -> b c n", n=NODES)
+            copy_on(engine, tok[(0, h)][:, 256 * u:256 * (u + 1), :], values)
+
+        def weave(engine, out, in_):
+            out, in_ = out.rearrange("b (c i) n -> b c n i", i=4), in_.rearrange("b n (c i) -> b c n i", i=4)
+            if engine == "G":
+                nc.gpsimd.tensor_scalar(out=out, in0=in_, scalar1=1.0, scalar2=0.0, op0=ALU.mult, op1=ALU.add)
+            else:
+                copy_on(engine, out, in_)
+
+        def tok_b(h, engines):
+            tok[(1, h)] = work.tile([P, KP, NODES], BF16, name="tok", bufs=2, align_bytes=64)
+            for engine, c0, c1 in engines:
+                weave(engine, tok[(1, h)][:, c0:c1, :], db[h][:, :, c0:c1])
+
+        def quant_tok(a, h):
+            quantize(tok_q[(a, h)], 0, E5, tok[(a, h)][:].rearrange("b c n -> b (c n)"))
+
+        def feat_b_pe(h, q, tag):
+            bank = psum.tile([P, 2, 4, P], BF16, name=tag, bufs=2)
+            for r in range(2):
+                for t in range(4):
+                    nc.tensor.transpose(bank[:, r, t, :], db[h][:, 2 * q + r, P * t:P * (t + 1)], ident16[:])
+            return bank
+
+        def feat_b_out(h, q, bank, engine):
+            if q == 0:
+                feat[(1, h)] = work.tile([P, NODES, P, 4], BF16, name="feat", bufs=3, align_bytes=64)
+            copy_on(engine, feat[(1, h)][:, 2 * q:2 * q + 2], bank[:].rearrange("p r t b -> p r b t"))
+
+        def weave_f(x, engine):
+            tile = work.tile([P, KP, NODES], BF16, name="dz2t", bufs=2, align_bytes=64)
+            weave(engine, tile[:], raw[("f", x)][:])
+            release(("f", x))
+            return tile
+
+        def out1_pe(a, h, m, tag, bufs):
+            bank = psum.tile([P, KP], F32, name=tag, bufs=bufs)
+            mx(bank, f_q[m // 4], P * (m % 4), E4, tok_q[(a, h)], E5, True, True)
+            return bank
+
+        def out1_out(a, h, m, bank, engine):
+            stage = work.tile([P, KP], F32, name="raw", bufs=RAW_BUFS)
+            if a == 0:
+                copy_on(engine, stage[:].rearrange("c (p u e) -> c p u e", u=2, e=2), bank[:].rearrange("c (u p e) -> c p u e", u=2, e=2))
+            else:
+                copy_on(engine, stage[:].rearrange("c (p t) -> c p t", t=4), bank[:].rearrange("c (t p) -> c p t", t=4))
+            nc.sync.dma_start(out=out_1[C * a + P * m:C * a + P * (m + 1), KP * h:KP * (h + 1)], in_=stage[:])
+
+        def out0_pe(n, x, h, bank):
+            for a in range(2):
+                mx(bank, feat_q[(a, h)], P * n, E5, w1_q[(a, x, h)], E4, (h, a) == (0, 0), (h, a) == (1, 1))
+
+        def out0_out(n, x, bank, engine):
+            stage = work.tile([P, KP], F32, name="raw", bufs=RAW_BUFS)
+            copy_on(engine, stage[:].rearrange("b (m r) -> b m r", r=4), bank[:].rearrange("b (r m) -> b m r", r=4))
+            nc.sync.dma_start(out=out_0[:, n, KP * x:KP * (x + 1)], in_=stage[:])
+
+        pump()
+        mask2(0, 0, "S")
+        for g in range(2):
+            bank = turn_pe(("g", 0), g)
+            turn_out(("g", 0), g, bank, "S")
+        mask2(0, 1, "V")
+        turn2(0, 0)
+        turn2(0, 1)
+
+        pending = []
+        f_woven = {}
+        out1_left = [(a, 0, m) for a in (1, 0) for m in range(8)]
+        spare = ["tz", "misc"]
+        count = 0
+        for tick in range(18):
+            u_p = tick - 2
+            u_x = tick - 1
+            first = tick < 8
+            tick_jobs = [job for job in jobs if job_tick[job] == tick]
+            if tick == 1:
+                make_dz2(1, 0, 0)
+                make_dz2(1, 0, 1)
+                for unit, g in tick_jobs:
+                    pending.append((unit, g, turn_out(unit, g, turn_pe(unit, g), "S")))
+                make_dz2(1, 1, 0)
+                make_dz2(1, 1, 1)
+                for job in pending:
+                    turn_quant(*job)
+                pending = []
+                tick_jobs = []
+            turned = [turn_pe(unit, g, spare[k % 2]) for k, (unit, g) in enumerate(tick_jobs[:EV_V]) if not first]
+            if tick + 1 < 8:
+                mask2(tick + 1, 0, "S")
+            if tick == 10:
+                turned = [back_a_pe(0, u, "tz") for u in range(2)] + [feat_b_pe(0, q, "misc") for q in range(2)]
+            if 0 <= u_x < 16 and u_x not in M1_V:
+                mask1(u_x, "S")
+            if u_p >= 0:
+                make_dp(u_p, 0)
+            if 0 <= u_x < 16:
+                make_dh(u_x, 0)
+            held = []
+            if tick >= 11:
+                for k in range(OUTS[tick - 11]):
+                    job = out1_left[0]
+                    out1_left.remove(job)
+                    held.append((job, out1_pe(*job, spare[count % 2], 2)))
+                    count = count + 1
+            if 0 <= u_x < 16:
+                make_dh(u_x, 1)
+            if first and tick != 1:
+                make_dz2(tick, 0, 0)
+            if tick - F_AT in (0, 1):
+                f_woven[tick - F_AT] = weave_f(tick - F_AT, F_ENG)
+            if u_p >= 0:
+                make_dp(u_p, 1)
+            if first and tick != 1:
+                make_dz2(tick, 0, 1)
+            if tick + 1 < 8 and tick + 1 not in M2_V:
+                mask2(tick + 1, 1, "S")
+            for k, (job, bank) in enumerate(held):
+                out1_out(*job, bank, "V" if k < OUT_V else "S")
+            if tick == 10:
+                tok_b(0, [(TB_ENG, 0, KP)])
+                for u in range(2):
+                    back_a_out(0, u, turned[u], T10[u])
+                for q in range(2):
+                    feat_b_out(0, q, turned[2 + q], T10[2 + q])
+                quant_feat(0, 0)
+                quant_tok(1, 0)
+            if tick == 11:
+                quant_tok(0, 0)
+                quant_feat(1, 0)
+            if first and tick != 1:
+                make_dz2(tick, 1, 0)
+                make_dz2(tick, 1, 1)
+            if tick + 1 < 8 and tick + 1 in M2_V:
+                mask2(tick + 1, 1, "V")
+            if first or not tick_jobs:
+                for unit, g, stage in pending:
+                    turn_quant(unit, g, stage)
+                pending = []
+            for k, (unit, g) in enumerate(tick_jobs):
+                if len(pending) == WST:
+                    turn_quant(*pending[0])
+                    pending = pending[1:]
+                bank = turned[k] if k < len(turned) else turn_pe(unit, g, "misc" if first else spare[k % 2])
+                stage = turn_out(unit, g, bank, "V" if not first and k < EV_V else "S")
+                if unit[0] != "g":
+                    pending.append((unit, g, stage))
+            if not first:
+                for unit, g, stage in pending[:len(pending) - 2]:
+                    turn_quant(unit, g, stage)
+                pending = pending[len(pending) - 2:]
+            if 0 <= u_x < 16 and u_x in M1_V:
+                mask1(u_x, "V")
+            if tick + 1 < 8:
+                turn2(tick + 1, 0)
+            if u_p >= 0 and u_p % 2 == 1 and u_p < 15:
+                h, i = u_p // 8, (u_p % 8) // 2
+                bank = sum_da_pe(h, i)
+                sum_da_out(h, i, bank, "S")
+            if u_p == 14:
+                last_bank = psum.tile([P, 4, P], F32, name="da", bufs=1)
+            if u_p >= 14:
+                for j in range(2):
+                    sum_da_node(1, 3, 2 * (u_p % 2) + j, last_bank)
+            if tick + 1 < 8:
+                turn2(tick + 1, 1)
+            if first:
+                quant_dz2(tick)
+            if tick - F_AT in (0, 1):
+                quantize(f_q[tick - F_AT], 0, E4, f_woven[tick - F_AT][:].rearrange("b c n -> b (c n)"))
+
+        for j in range(2):
+            add_db(15, j, nc.vector)
+        sum_da_out(1, 3, last_bank, "S")
+        tok_b(1, [("S", 0, TB_SPLIT), ("V", TB_SPLIT, KP)])
+        held = [(job, out1_pe(*job, "dh", 3)) for job in out1_left]
+        quant_tok(1, 1)
+        a_banks = [back_a_pe(1, u, "tz") for u in range(2)]
+        b_banks = [feat_b_pe(1, q, "misc") for q in range(2)]
+        out1_out(*held[0][0], held[0][1], "S")
+        for u in range(2):
+            back_a_out(1, u, a_banks[u], "VS"[u])
+        quant_feat(0, 1)
+        tiles1 = [(a, 1, m) for a in (1, 0) for m in range(8)]
+        tiles0 = [(n, x) for n in range(NODES) for x in range(2)]
+        ring = [("da", 1), ("dh", 3), ("dh", 3), ("dh", 3)]
+        opened = {}
+        for k, job in enumerate(tiles1):
+            if k < len(held) - 1:
+                out1_out(*held[k + 1][0], held[k + 1][1], "S")
+            bank = out1_pe(*job, *ring[k % 4])
+            if k == 0:
+                quant_tok(0, 1)
+                for q in range(2):
+                    feat_b_out(1, q, b_banks[q], "V")
+                quant_feat(1, 1)
+            out1_out(*job, bank, "S" if k < S_ONLY or k % 2 == 1 else "V")
+            if k % 4 == 3:
+                n, x = tiles0[k // 4]
+                opened[(n, x)] = psum.tile([P, KP], F32, name=spare[(k // 8) % 2], bufs=2)
+                out0_pe(n, x, 0, opened[(n, x)])
+        for k, (n, x) in enumerate(tiles0):
+            if (n, x) not in opened:
+                tag, bufs = ring[k % 4]
+                opened[(n, x)] = psum.tile([P, KP], F32, name=tag, bufs=bufs)
+                out0_pe(n, x, 0, opened[(n, x)])
+            out0_pe(n, x, 1, opened[(n, x)])
+            out0_out(n, x, opened[(n, x)], "SV"[k % 2])

@@ -21,24 +21,31 @@ TINY = 2.0 ** -126
 FLOPS = 2 * 2048 * C * C + 2 * 2 * 512 * 2048 * C
 BYTES = 2 * (512 * C * 2 + 3 * C * C) + 4 * (2 * 2048 * C + 512 * C + 2048 * C)
 
-RAW_BUFS = 17
-JOBS = (0, 4, 2, 0, 2, 2, 2, 2, 6, 6)
-OUTS = (2, 2, 2, 2, 3, 2, 0)
+RAW_BUFS = 18
+JOBS = (0, 4, 2, 2, 2, 2, 4, 2, 4, 4)
+OUTS = (2, 2, 2, 3, 2, 3, 2)
 OUT_V = 1
 M1_V = (0, 3, 5)
 M2_V = (1,)
-ADD_G = True
 F_AT = 2
 F_ENG = "G"
 F_LEAD = 0.95
 Z1_LEAD = 0.0
 W_LEAD = 0.5
-TB_SPLIT = 160
-EV_V = 2
+TB_SPLIT = 128
 TB_ENG = "V"
-T10 = "SSSS"
-S_ONLY = 6
-WST = 5
+S_ONLY = 16
+EV8 = "SS"
+FB_AT = 12
+FB_ENG = "SS"
+WST = 3
+W1_LATE = 4
+OPEN_AT = 8
+LATE_N = 2
+EVAC_FIRST = 0
+T2_FIRST = 0
+DP_BUFS = 9
+S1_BUFS = 3
 
 
 def tile_nonlocalmp_pa_v_kernel(tc, F, W1, b1, W2, b2, z1, z2, grad_out, out_0, out_1):
@@ -100,8 +107,9 @@ def tile_nonlocalmp_pa_v_kernel(tc, F, W1, b1, W2, b2, z1, z2, grad_out, out_0, 
                 return rows4(W1, key[1], key[2])
             return F[:, :, KP * key[1]:KP * (key[1] + 1)]
 
-        turn_units = [("w2", 0, 0), ("w2", 0, 1), ("g", 1), ("w2", 1, 0), ("w2", 1, 1)] + [("w1", x, q) for x in range(4) for q in range(2)]
-        jobs = [(u, g) for u in turn_units for g in range(2)]
+        turn_units = [("g", 1)] + [(w, x, q) for w, blocks in (("w2", 2), ("w1", 4)) for x in range(blocks) for q in range(2)]
+        jobs = [(("w2", 0, q), g) for g in range(2) for q in range(2)] + [(("g", 1), g) for g in range(2)]
+        jobs.extend([((w, x, q), g) for w, x in [("w2", 1)] + [("w1", x) for x in range(4)] for g in range(2) for q in range(2)])
         slots = [t for t, n in enumerate(JOBS) for k in range(n)]
         job_tick = dict(zip(jobs, slots))
         need = [(-3, ("z2", 0, 0)), (-2.5, ("g", 0)), (-2, ("z2", 0, 1))]
@@ -136,21 +144,25 @@ def tile_nonlocalmp_pa_v_kernel(tc, F, W1, b1, W2, b2, z1, z2, grad_out, out_0, 
                 release(unit)
             return bank
 
+        wstage = {}
+
         def turn_out(unit, g, bank, engine):
             if unit[0] == "g":
                 dst = g_t[(g, unit[1])]
             else:
-                dst = work.tile([P, 2, P, 4], BF16, name="wstage", bufs=WST, align_bytes=64)
+                if unit[2] == 0:
+                    wstage[unit[:2] + (g,)] = work.tile([P, 4, P, 4], BF16, name="wstage", bufs=WST, align_bytes=64)
+                dst = wstage[unit[:2] + (g,)][:, 2 * unit[2]:2 * unit[2] + 2]
             words = dst[:].rearrange("p r m t -> p (r m t)").bitcast(F32).rearrange("p (r m u) -> p r m u", r=2, u=2)
             copy_on(engine, words, bank[:].rearrange("p r u m -> p r m u"))
             return dst
 
-        def turn_quant(unit, g, stage):
+        def turn_quant(unit, g):
             if unit[0] == "w2":
                 store = w2_q[(unit[1], g)]
             else:
                 store = w1_q[(unit[1] // 2, unit[1] % 2, g)]
-            quantize(store, 256 * unit[2], E4, stage[:].rearrange("p r m t -> p (r m t)"))
+            quantize(store, 0, E4, wstage[unit[:2] + (g,)][:].rearrange("p r m t -> p (r m t)"))
 
         def sign_of(engine, out, in_):
             if engine == "S":
@@ -201,7 +213,7 @@ def tile_nonlocalmp_pa_v_kernel(tc, F, W1, b1, W2, b2, z1, z2, grad_out, out_0, 
             dh[(u, j)] = bank
 
         def mask1(u, engine):
-            tile = work.tile([P, 2, 4, P], F32, name="sign1", bufs=3)
+            tile = work.tile([P, 2, 4, P], BF16, name="sign1", bufs=S1_BUFS)
             sign_of(engine, tile[:].rearrange("b j t p -> b j p t"), raw[("z1", u)][:].rearrange("b j (p t) -> b j p t", t=4))
             sign1[u] = tile
             release(("z1", u))
@@ -209,7 +221,7 @@ def tile_nonlocalmp_pa_v_kernel(tc, F, W1, b1, W2, b2, z1, z2, grad_out, out_0, 
         def make_dp(u, j):
             h, s = divmod(u, 8)
             i, node = s // 2, 2 * (s % 2) + j
-            tile = work.tile([P, KP], F32, name="dp", bufs=9)
+            tile = work.tile([P, KP], F32, name="dp", bufs=DP_BUFS)
             nc.vector.scalar_tensor_tensor(out=tile[:], in0=sign1[u][:, j].rearrange("b t p -> b (t p)"), scalar=SLOPE, in1=dh[(u, j)][:],
                                            op0=ALU.max, op1=ALU.mult)
             dp[(h, i, node)] = tile
@@ -265,11 +277,10 @@ def tile_nonlocalmp_pa_v_kernel(tc, F, W1, b1, W2, b2, z1, z2, grad_out, out_0, 
             copy_on(engine, tok[(0, h)][:, 256 * u:256 * (u + 1), :], values)
 
         def weave(engine, out, in_):
-            out, in_ = out.rearrange("b (c i) n -> b c n i", i=4), in_.rearrange("b n (c i) -> b c n i", i=4)
             if engine == "G":
-                nc.gpsimd.tensor_scalar(out=out, in0=in_, scalar1=1.0, scalar2=0.0, op0=ALU.mult, op1=ALU.add)
+                nc.gpsimd.tensor_scalar(out=out, in0=in_.rearrange("b n c -> b c n"), scalar1=1.0, scalar2=0.0, op0=ALU.mult, op1=ALU.add)
             else:
-                copy_on(engine, out, in_)
+                copy_on(engine, out.rearrange("b (c i) n -> b c n i", i=4), in_.rearrange("b n (c i) -> b c n i", i=4))
 
         def tok_b(h, engines):
             tok[(1, h)] = work.tile([P, KP, NODES], BF16, name="tok", bufs=2, align_bytes=64)
@@ -329,31 +340,35 @@ def tile_nonlocalmp_pa_v_kernel(tc, F, W1, b1, W2, b2, z1, z2, grad_out, out_0, 
         turn2(0, 1)
 
         pending = []
+        late = []
         f_woven = {}
         out1_left = [(a, 0, m) for a in (1, 0) for m in range(8)]
         spare = ["tz", "misc"]
         count = 0
+
+        def run_jobs(some, tags, engines):
+            for k, (unit, g) in enumerate(some):
+                turn_out(unit, g, turn_pe(unit, g, tags[k % len(tags)]), engines[k % len(engines)])
+            return [(unit, g) for unit, g in some if unit[0] != "g" and unit[2] == 1]
+
         for tick in range(18):
             u_p = tick - 2
             u_x = tick - 1
             first = tick < 8
             tick_jobs = [job for job in jobs if job_tick[job] == tick]
+            staged = []
             if tick == 1:
                 make_dz2(1, 0, 0)
                 make_dz2(1, 0, 1)
-                for unit, g in tick_jobs:
-                    pending.append((unit, g, turn_out(unit, g, turn_pe(unit, g), "S")))
+                staged = run_jobs(tick_jobs, ["misc"], "S")
                 make_dz2(1, 1, 0)
+                turn_quant(*staged[0])
                 make_dz2(1, 1, 1)
-                for job in pending:
-                    turn_quant(*job)
-                pending = []
+                turn_quant(*staged[1])
+                staged = []
                 tick_jobs = []
-            turned = [turn_pe(unit, g, spare[k % 2]) for k, (unit, g) in enumerate(tick_jobs[:EV_V]) if not first]
             if tick + 1 < 8:
                 mask2(tick + 1, 0, "S")
-            if tick == 10:
-                turned = [back_a_pe(0, u, "tz") for u in range(2)] + [feat_b_pe(0, q, "misc") for q in range(2)]
             if 0 <= u_x < 16 and u_x not in M1_V:
                 mask1(u_x, "S")
             if u_p >= 0:
@@ -367,8 +382,6 @@ def tile_nonlocalmp_pa_v_kernel(tc, F, W1, b1, W2, b2, z1, z2, grad_out, out_0, 
                     out1_left.remove(job)
                     held.append((job, out1_pe(*job, spare[count % 2], 2)))
                     count = count + 1
-            if 0 <= u_x < 16:
-                make_dh(u_x, 1)
             if first and tick != 1:
                 make_dz2(tick, 0, 0)
             if tick - F_AT in (0, 1):
@@ -377,46 +390,50 @@ def tile_nonlocalmp_pa_v_kernel(tc, F, W1, b1, W2, b2, z1, z2, grad_out, out_0, 
                 make_dp(u_p, 1)
             if first and tick != 1:
                 make_dz2(tick, 0, 1)
-            if tick + 1 < 8 and tick + 1 not in M2_V:
+            if tick + 1 < 8 and tick + 1 not in M2_V and not EVAC_FIRST:
                 mask2(tick + 1, 1, "S")
             for k, (job, bank) in enumerate(held):
-                out1_out(*job, bank, "V" if k < OUT_V else "S")
+                out1_out(*job, bank, "V" if k < OUT_V and tick < 17 else "S")
             if tick == 10:
+                turned = [back_a_pe(0, u, "tz") for u in range(2)]
                 tok_b(0, [(TB_ENG, 0, KP)])
                 for u in range(2):
-                    back_a_out(0, u, turned[u], T10[u])
-                for q in range(2):
-                    feat_b_out(0, q, turned[2 + q], T10[2 + q])
-                quant_feat(0, 0)
+                    back_a_out(0, u, turned[u], "S")
                 quant_tok(1, 0)
             if tick == 11:
                 quant_tok(0, 0)
-                quant_feat(1, 0)
+                quant_feat(0, 0)
+            staged.extend(run_jobs(tick_jobs[:2], ["misc"] if first else spare, "S" if first else EV8))
+            if tick + 1 < 8 and tick + 1 not in M2_V and EVAC_FIRST:
+                mask2(tick + 1, 1, "S")
+            if tick + 1 < 8:
+                turn2(tick + 1, 0)
+            if 0 <= u_x < 16:
+                make_dh(u_x, 1)
             if first and tick != 1:
                 make_dz2(tick, 1, 0)
                 make_dz2(tick, 1, 1)
             if tick + 1 < 8 and tick + 1 in M2_V:
                 mask2(tick + 1, 1, "V")
-            if first or not tick_jobs:
-                for unit, g, stage in pending:
-                    turn_quant(unit, g, stage)
-                pending = []
-            for k, (unit, g) in enumerate(tick_jobs):
-                if len(pending) == WST:
-                    turn_quant(*pending[0])
-                    pending = pending[1:]
-                bank = turned[k] if k < len(turned) else turn_pe(unit, g, "misc" if first else spare[k % 2])
-                stage = turn_out(unit, g, bank, "V" if not first and k < EV_V else "S")
-                if unit[0] != "g":
-                    pending.append((unit, g, stage))
-            if not first:
-                for unit, g, stage in pending[:len(pending) - 2]:
-                    turn_quant(unit, g, stage)
-                pending = pending[len(pending) - 2:]
+            for job in pending:
+                if job[0][0] == "w1" and job[0][1] >= W1_LATE:
+                    late.append(job)
+                else:
+                    turn_quant(*job)
+            if tick >= 8:
+                for job in late[:LATE_N]:
+                    turn_quant(*job)
+                late = late[LATE_N:]
             if 0 <= u_x < 16 and u_x in M1_V:
                 mask1(u_x, "V")
-            if tick + 1 < 8:
-                turn2(tick + 1, 0)
+            if tick + 1 < 8 and T2_FIRST:
+                turn2(tick + 1, 1)
+            staged.extend(run_jobs(tick_jobs[2:], ["misc"] if first else spare, "S"))
+            pending = staged
+            if tick - FB_AT in (0, 2):
+                q = (tick - FB_AT) // 2
+                feat_b_out(0, q, feat_b_pe(0, q, spare[count % 2]), FB_ENG[q])
+                count = count + 1
             if u_p >= 0 and u_p % 2 == 1 and u_p < 15:
                 h, i = u_p // 8, (u_p % 8) // 2
                 bank = sum_da_pe(h, i)
@@ -426,7 +443,7 @@ def tile_nonlocalmp_pa_v_kernel(tc, F, W1, b1, W2, b2, z1, z2, grad_out, out_0, 
             if u_p >= 14:
                 for j in range(2):
                     sum_da_node(1, 3, 2 * (u_p % 2) + j, last_bank)
-            if tick + 1 < 8:
+            if tick + 1 < 8 and not T2_FIRST:
                 turn2(tick + 1, 1)
             if first:
                 quant_dz2(tick)
@@ -437,31 +454,32 @@ def tile_nonlocalmp_pa_v_kernel(tc, F, W1, b1, W2, b2, z1, z2, grad_out, out_0, 
             add_db(15, j, nc.vector)
         sum_da_out(1, 3, last_bank, "S")
         tok_b(1, [("S", 0, TB_SPLIT), ("V", TB_SPLIT, KP)])
-        held = [(job, out1_pe(*job, "dh", 3)) for job in out1_left]
         quant_tok(1, 1)
-        a_banks = [back_a_pe(1, u, "tz") for u in range(2)]
-        b_banks = [feat_b_pe(1, q, "misc") for q in range(2)]
-        out1_out(*held[0][0], held[0][1], "S")
+        a_banks = [back_a_pe(1, u, spare[(count + u) % 2]) for u in range(2)]
+        b_banks = [feat_b_pe(1, q, spare[(count + q) % 2]) for q in range(2)]
         for u in range(2):
-            back_a_out(1, u, a_banks[u], "VS"[u])
-        quant_feat(0, 1)
+            back_a_out(1, u, a_banks[u], "SV"[u])
         tiles1 = [(a, 1, m) for a in (1, 0) for m in range(8)]
-        tiles0 = [(n, x) for n in range(NODES) for x in range(2)]
-        ring = [("da", 1), ("dh", 3), ("dh", 3), ("dh", 3)]
+        tiles0 = [(n, x) for x in range(2) for n in range(NODES)]
+        ring = [("dh", 3), ("dh", 3), ("dh", 3), ("da", 1)]
+        late = sorted(late, key=lambda job: (job[1], job[0][1] % 2))
+        chain = [lambda: quant_tok(0, 1), lambda: feat_b_out(1, 0, b_banks[0], "V"), lambda: feat_b_out(1, 1, b_banks[1], "V"), lambda: quant_feat(1, 0)]
+        chain.extend([lambda job=job: turn_quant(*job) for job in late if job[1] == 0])
+        n_first = len(chain)
+        chain.extend([lambda: quant_feat(0, 1), lambda: quant_feat(1, 1)])
+        chain.extend([lambda job=job: turn_quant(*job) for job in late if job[1] == 1])
+        for step in chain[:n_first]:
+            step()
         opened = {}
         for k, job in enumerate(tiles1):
-            if k < len(held) - 1:
-                out1_out(*held[k + 1][0], held[k + 1][1], "S")
             bank = out1_pe(*job, *ring[k % 4])
-            if k == 0:
-                quant_tok(0, 1)
-                for q in range(2):
-                    feat_b_out(1, q, b_banks[q], "V")
-                quant_feat(1, 1)
+            if k == 8:
+                for step in chain[n_first:]:
+                    step()
             out1_out(*job, bank, "S" if k < S_ONLY or k % 2 == 1 else "V")
-            if k % 4 == 3:
-                n, x = tiles0[k // 4]
-                opened[(n, x)] = psum.tile([P, KP], F32, name=spare[(k // 8) % 2], bufs=2)
+            if k >= OPEN_AT and (k - OPEN_AT) % 2 == 0 and len(opened) < 4:
+                n, x = tiles0[len(opened)]
+                opened[(n, x)] = psum.tile([P, KP], F32, name=spare[(count + len(opened)) % 2], bufs=2)
                 out0_pe(n, x, 0, opened[(n, x)])
         for k, (n, x) in enumerate(tiles0):
             if (n, x) not in opened:
@@ -469,4 +487,4 @@ def tile_nonlocalmp_pa_v_kernel(tc, F, W1, b1, W2, b2, z1, z2, grad_out, out_0, 
                 opened[(n, x)] = psum.tile([P, KP], F32, name=tag, bufs=bufs)
                 out0_pe(n, x, 0, opened[(n, x)])
             out0_pe(n, x, 1, opened[(n, x)])
-            out0_out(n, x, opened[(n, x)], "SV"[k % 2])
+            out0_out(n, x, opened[(n, x)], "VS"[k % 2])

@@ -7,8 +7,8 @@ F32 = mybir.dt.float32
 BF16 = mybir.dt.bfloat16
 U32 = mybir.dt.uint32
 U8 = mybir.dt.uint8
-E4 = mybir.dt.float8_e4m3fn_x4
-E5 = mybir.dt.float8_e5m2_x4
+E4M3 = mybir.dt.float8_e4m3fn_x4
+E5M2 = mybir.dt.float8_e5m2_x4
 ALU = mybir.AluOpType
 ACT = mybir.ActivationFunctionType
 
@@ -16,36 +16,18 @@ P = 128
 NODES = 4
 C = 1024
 KP = 512
+STEPS = 8
 SLOPE = 0.2
 TINY = 2.0 ** -126
-FLOPS = 2 * 2048 * C * C + 2 * 2 * 512 * 2048 * C
-BYTES = 2 * (512 * C * 2 + 3 * C * C) + 4 * (2 * 2048 * C + 512 * C + 2048 * C)
+FLOPS = 2 * P * NODES * NODES * C * C + 2 * (2 * P * NODES * 2 * C * C)
+BYTES = 2 * (2 * P * NODES * C + 3 * C * C) + 4 * (2 * P * NODES * NODES * C + P * NODES * C + 2 * C * C)
 
-RAW_BUFS = 18
-JOBS = (0, 4, 2, 2, 2, 2, 4, 2, 4, 4)
-OUTS = (2, 2, 2, 3, 2, 3, 2)
-OUT_V = 1
-M1_V = (0, 3, 5)
-M2_V = (1,)
-F_AT = 2
-F_ENG = "G"
-F_LEAD = 0.95
-Z1_LEAD = 0.0
-W_LEAD = 0.5
-TB_SPLIT = 128
-TB_ENG = "V"
-S_ONLY = 16
-EV8 = "SS"
-FB_AT = 12
-FB_ENG = "SS"
-WST = 3
-W1_LATE = 4
-OPEN_AT = 8
-LATE_N = 2
-EVAC_FIRST = 0
-T2_FIRST = 0
+BIG_BUFS = 5
+SMALL_BUFS = 8
 DP_BUFS = 9
-S1_BUFS = 3
+SCALAR_COLUMNS = 176
+DB_TURN_TICK = 13
+OPEN_AFTER = 6
 
 
 def tile_nonlocalmp_pa_v_kernel(tc, F, W1, b1, W2, b2, z1, z2, grad_out, out_0, out_1):
@@ -61,430 +43,424 @@ def tile_nonlocalmp_pa_v_kernel(tc, F, W1, b1, W2, b2, z1, z2, grad_out, out_0, 
         make_identity(nc, ident32[:])
         make_identity(nc, ident16[:])
 
-        def mx_store(name, cols):
-            codes = keep.tile([P, cols], U32, name=name + "_codes", align_bytes=64)
-            scales = keep.tile([P, cols], U8, name=name + "_scales", align_bytes=64)
+        bank_count = {"dh": 3, "signs": 2, "turn": 2, "da": 1}
+
+        def new_bank(role, shape, dtype=F32):
+            return psum.tile(shape, dtype, name=role, bufs=bank_count[role])
+
+        def mx_operand(name):
+            codes = keep.tile([P, KP], U32, name=name + "_codes", align_bytes=64)
+            scales = keep.tile([P, KP], U8, name=name + "_scales", align_bytes=64)
             return codes, scales
 
-        dz2_q = [mx_store("dz2q%d" % s, KP) for s in range(8)]
-        w2_q = {(h, g): mx_store("w2q%d%d" % (h, g), KP) for h in range(2) for g in range(2)}
-        w1_q = {(a, x, h): mx_store("w1q%d%d%d" % (a, x, h), KP) for a in range(2) for x in range(2) for h in range(2)}
-        f_q = [mx_store("fq%d" % x, KP) for x in range(2)]
-        feat_q = {(a, h): mx_store("featq%d%d" % (a, h), KP) for a in range(2) for h in range(2)}
-        tok_q = {(a, h): mx_store("tokq%d%d" % (a, h), KP) for a in range(2) for h in range(2)}
-        g_t = {(g, q): keep.tile([P, 2, P, 4], BF16, name="gt%d%d" % (g, q)) for g in range(2) for q in range(2)}
+        two = range(2)
+        dz2_mx = [mx_operand("dz2_%d" % s) for s in range(STEPS)]
+        w2_mx = {(h, g): mx_operand("w2_%d%d" % (h, g)) for h in two for g in two}
+        w1_mx = {(a, x, h): mx_operand("w1_%d%d%d" % (a, x, h)) for a in two for x in two for h in two}
+        f_mx = [mx_operand("f_%d" % x) for x in two]
+        dz1_feat_mx = {(a, h): mx_operand("dz1f_%d%d" % (a, h)) for a in two for h in two}
+        dz1_tok_mx = {(a, h): mx_operand("dz1t_%d%d" % (a, h)) for a in two for h in two}
+        grad_t = {(g, q): keep.tile([P, 2, P, 4], BF16, name="grad_t%d%d" % (g, q)) for g in two for q in two}
 
-        def quantize(store, c0, fmt, src):
-            n = src.shape[1] // 4
-            nc.vector.quantize_mx(out=store[0][:, c0:c0 + n].bitcast(fmt), scales=store[1][:, c0:c0 + n], in_=src)
+        def quantize(operand, fmt, tile, pattern):
+            nc.vector.quantize_mx(out=operand[0][:].bitcast(fmt), scales=operand[1][:], in_=tile[:].rearrange(pattern))
 
-        def mx(bank, lhs, l0, lfmt, rhs, rfmt, start, stop):
-            nc.tensor.matmul_mx(out=bank[:], lhsT=lhs[0][:, l0:l0 + P].bitcast(lfmt), lhsT_scale=lhs[1][:, l0:l0 + P],
-                                rhs=rhs[0][:].bitcast(rfmt), rhs_scale=rhs[1][:], start=start, stop=stop)
+        def mx_pass(bank, lhs, column, lhs_fmt, rhs, rhs_fmt, start, stop):
+            cols = slice(column, column + P)
+            nc.tensor.matmul_mx(out=bank[:], lhsT=lhs[0][:, cols].bitcast(lhs_fmt), lhsT_scale=lhs[1][:, cols],
+                                rhs=rhs[0][:].bitcast(rhs_fmt), rhs_scale=rhs[1][:], start=start, stop=stop)
 
         def copy_on(engine, out, in_):
-            if engine == "S":
+            if engine == "scalar":
                 nc.scalar.copy(out=out, in_=in_)
             else:
                 nc.vector.tensor_copy(out=out, in_=in_)
 
-        def rows4(w, x, q):
-            return w[KP * x:KP * (x + 1), :].rearrange("(m r) k -> m r k", r=4)[:, 2 * q:2 * q + 2, :]
+        weight_blocks = [("w2", 0), ("w2", 1)] + [("w1", x) for x in range(4)]
+
+        def turns_of(block):
+            return [(block, q, g) for g in two for q in two]
+
+        later_turns = [(("grad", 1), 0, g) for g in two] + [turn for block in weight_blocks[1:] for turn in turns_of(block)]
+        later_ticks = [t for t in range(3, 10) for k in range(2 if t % 2 == 1 and t < 9 else 4)]
+        turn_tick = dict(zip(turns_of(weight_blocks[0]) + later_turns, [1] * 4 + later_ticks))
 
         def source(key):
-            kind = key[0]
+            kind, n = key
+            if kind == "z2_first":
+                return z2[:, 0, 0:2, KP * n:KP * (n + 1)]
             if kind == "z2":
-                s, g = key[1:]
-                return z2[:, s // 2, 2 * (s % 2):2 * (s % 2) + 2, KP * g:KP * (g + 1)]
+                return z2[:, n // 2, 2 * (n % 2):2 * (n % 2) + 2, :]
             if kind == "z1":
-                h, s = divmod(key[1], 8)
+                h, s = divmod(n, STEPS)
                 return z1[:, s // 2, 2 * (s % 2):2 * (s % 2) + 2, KP * h:KP * (h + 1)]
-            if kind == "g":
-                return grad_out[:, 2 * key[1]:2 * key[1] + 2, :]
-            if kind == "w2":
-                return rows4(W2, key[1], key[2])
-            if kind == "w1":
-                return rows4(W1, key[1], key[2])
-            return F[:, :, KP * key[1]:KP * (key[1] + 1)]
+            if kind == "grad":
+                return grad_out[:, 2 * n:2 * n + 2, :]
+            if kind == "f":
+                return F
+            return (W2 if kind == "w2" else W1)[KP * n:KP * (n + 1), :].rearrange("(m r) k -> m r k", r=4)
 
-        turn_units = [("g", 1)] + [(w, x, q) for w, blocks in (("w2", 2), ("w1", 4)) for x in range(blocks) for q in range(2)]
-        jobs = [(("w2", 0, q), g) for g in range(2) for q in range(2)] + [(("g", 1), g) for g in range(2)]
-        jobs.extend([((w, x, q), g) for w, x in [("w2", 1)] + [("w1", x) for x in range(4)] for g in range(2) for q in range(2)])
-        slots = [t for t, n in enumerate(JOBS) for k in range(n)]
-        job_tick = dict(zip(jobs, slots))
-        need = [(-3, ("z2", 0, 0)), (-2.5, ("g", 0)), (-2, ("z2", 0, 1))]
-        need.extend([(s - 1.2 + 0.1 * g, ("z2", s, g)) for s in range(1, 8) for g in range(2)])
-        need.extend([(u + 0.9 - Z1_LEAD, ("z1", u)) for u in range(16)])
-        need.extend([(job_tick[(u, 0)] - W_LEAD, u) for u in turn_units])
-        need.extend([(F_AT - F_LEAD + x, ("f", x)) for x in range(2)])
-        order = [key for rank, key in sorted(need)]
-        raw = {}
-        done = set()
+        load_order = [("z2_first", 0), ("grad", 0), ("z2_first", 1)]
+        for tick in range(1, 2 * STEPS + 1):
+            load_order.extend([("z2", tick)] if tick == 1 else [])
+            load_order.extend([block for block in weight_blocks if turn_tick[(block, 0, 0)] == tick])
+            load_order.extend([("z2", tick + 1)] if tick + 1 < STEPS else [])
+            load_order.append(("z1", tick - 1))
+            load_order.extend({1: [("f", 0)], 2: [("grad", 1)]}.get(tick, []))
+        depth = {"big": BIG_BUFS, "small": SMALL_BUFS}
+        size = {key: "small" if key[0] in ("z2_first", "z1", "grad") else "big" for key in load_order}
+        loaded = {}
+        used_up = set()
 
-        def pump():
-            while len(raw) < len(order) and (len(raw) < RAW_BUFS or order[len(raw) - RAW_BUFS] in done):
-                key = order[len(raw)]
+        def issue_loads():
+            for key in load_order[len(loaded):]:
+                earlier = [other for other in loaded if size[other] == size[key]]
+                if len(earlier) >= depth[size[key]] and earlier[len(earlier) - depth[size[key]]] not in used_up:
+                    return
                 src = source(key)
-                tile = work.tile(list(src.shape), src.dtype, name="raw", bufs=RAW_BUFS)
-                nc.sync.dma_start(out=tile[:], in_=src)
-                raw[key] = tile
+                loaded[key] = work.tile(list(src.shape), src.dtype, name=size[key], bufs=depth[size[key]])
+                nc.sync.dma_start(out=loaded[key][:], in_=src)
 
         def release(key):
-            done.add(key)
-            pump()
+            used_up.add(key)
+            issue_loads()
 
-        def turn_pe(unit, g, tag="misc"):
-            words = raw[unit][:].rearrange("p r k -> p (r k)").bitcast(F32)
-            bank = psum.tile([P, 2, 2, P], F32, name=tag, bufs=2)
-            for r in range(2):
-                for u in range(2):
-                    w0 = KP * r + 256 * g
-                    nc.tensor.transpose(bank[:, r, u, :], words[:, w0 + u:w0 + 256:2], ident32[:])
-            if g == 1:
-                release(unit)
-            return bank
+        turned = {}
 
-        wstage = {}
-
-        def turn_out(unit, g, bank, engine):
-            if unit[0] == "g":
-                dst = g_t[(g, unit[1])]
+        def turn(block, q, g, role):
+            is_grad = block[0] == "grad"
+            words = loaded[block][:].rearrange("p r k -> p (r k)").bitcast(F32)
+            bank = new_bank(role, [P, 2, 2, P])
+            for r in two:
+                first = KP * (2 * q + r) + 256 * g
+                for u in two:
+                    nc.tensor.transpose(bank[:, r, u, :], words[:, first + u:first + 256:2], ident32[:])
+            if g == 1 and (is_grad or q == 1):
+                release(block)
+            if is_grad:
+                dst = grad_t[(g, block[1])][:]
             else:
-                if unit[2] == 0:
-                    wstage[unit[:2] + (g,)] = work.tile([P, 4, P, 4], BF16, name="wstage", bufs=WST, align_bytes=64)
-                dst = wstage[unit[:2] + (g,)][:, 2 * unit[2]:2 * unit[2] + 2]
-            words = dst[:].rearrange("p r m t -> p (r m t)").bitcast(F32).rearrange("p (r m u) -> p r m u", r=2, u=2)
-            copy_on(engine, words, bank[:].rearrange("p r u m -> p r m u"))
-            return dst
+                if q == 0:
+                    turned[(block, g)] = work.tile([P, 4, P, 4], BF16, name="turned", bufs=3, align_bytes=64)
+                dst = turned[(block, g)][:, 2 * q:2 * q + 2]
+            dst = dst.rearrange("p r m t -> p (r m t)").bitcast(F32).rearrange("p (r m u) -> p r m u", r=2, u=2)
+            nc.scalar.copy(out=dst, in_=bank[:].rearrange("p r u m -> p r m u"))
 
-        def turn_quant(unit, g):
-            if unit[0] == "w2":
-                store = w2_q[(unit[1], g)]
-            else:
-                store = w1_q[(unit[1] // 2, unit[1] % 2, g)]
-            quantize(store, 0, E4, wstage[unit[:2] + (g,)][:].rearrange("p r m t -> p (r m t)"))
+        def run_turns(turns, roles):
+            for k, (block, q, g) in enumerate(turns):
+                turn(block, q, g, roles[k % len(roles)])
+            return [(block, g) for block, q, g in turns if block[0] != "grad" and q == 1]
 
-        def sign_of(engine, out, in_):
-            if engine == "S":
+        def quantize_weight(block, g):
+            kind, n = block
+            operand = w2_mx[(n, g)] if kind == "w2" else w1_mx[(n // 2, n % 2, g)]
+            quantize(operand, E4M3, turned[(block, g)], "p r m t -> p (r m t)")
+
+        def sign_on(engine, out, in_):
+            if engine == "scalar":
                 nc.scalar.activation(out=out, in_=in_, func=ACT.Sign, bias=TINY)
             else:
                 nc.vector.tensor_scalar(out=out, in0=in_, scalar1=0.0, scalar2=None, op0=ALU.is_ge)
 
-        sign2 = {}
-        sign2_t = {}
-        dz2_t = {}
-        sign1 = {}
-        dh = {}
-        dp = {}
-        acc = {}
-        db = {}
-        feat = {}
-        tok = {}
+        sign2, sign2_t, dz2_t = {}, {}, {}
 
-        def mask2(s, g, engine):
-            tile = work.tile([P, 4, P, 2], BF16, name="sign2", bufs=3)
-            sign_of(engine, tile[:].rearrange("b t p j -> b p t j"), raw[("z2", s, g)][:].rearrange("b j (p t) -> b p t j", t=4))
-            sign2[(s, g)] = tile
-            release(("z2", s, g))
+        def make_sign2(s, g, engine):
+            key = ("z2_first", g) if s == 0 else ("z2", s)
+            z = loaded[key][:] if s == 0 else loaded[key][:, :, KP * g:KP * (g + 1)]
+            sign2[(s, g)] = work.tile([P, 4, P, 2], BF16, name="sign2", bufs=3)
+            sign_on(engine, sign2[(s, g)][:].rearrange("b t p j -> b p t j"), z.rearrange("b j (p t) -> b p t j", t=4))
+            if s == 0 or g == 1:
+                release(key)
 
-        def turn2(s, g):
+        def turn_sign2(s, g):
             words = sign2[(s, g)][:].rearrange("b t p j -> b (t p j)").bitcast(F32)
-            bank = psum.tile([P, 4, P], F32, name="tz", bufs=2)
+            sign2_t[(s, g)] = new_bank("signs", [P, 4, P])
             for t in range(4):
-                nc.tensor.transpose(bank[:, t, :], words[:, P * t:P * (t + 1)], ident32[:])
-            sign2_t[(s, g)] = bank
+                nc.tensor.transpose(sign2_t[(s, g)][:, t, :], words[:, P * t:P * (t + 1)], ident32[:])
 
         def make_dz2(s, g, j):
             if (g, j) == (0, 0):
-                dz2_t[s] = work.tile([P, 2, 2, P, 4], BF16, name="dz2t", bufs=2, align_bytes=64)
+                dz2_t[s] = work.tile([P, 2, 2, P, 4], BF16, name="dz2_t", bufs=2, align_bytes=64)
             signs = sign2_t[(s, g)][:].rearrange("p t b -> p (t b)").bitcast(BF16).rearrange("p (t b j) -> p j b t", t=4, j=2)
             i = s // 2
-            nc.vector.scalar_tensor_tensor(out=dz2_t[s][:, j, g], in0=signs[:, j], scalar=SLOPE, in1=g_t[(g, i // 2)][:, i % 2],
-                                           op0=ALU.max, op1=ALU.mult)
+            nc.vector.scalar_tensor_tensor(out=dz2_t[s][:, j, g], in0=signs[:, j], scalar=SLOPE,
+                                           in1=grad_t[(g, i // 2)][:, i % 2], op0=ALU.max, op1=ALU.mult)
 
-        def quant_dz2(s):
-            quantize(dz2_q[s], 0, E5, dz2_t[s][:].rearrange("p j g b t -> p (j g b t)"))
+        def quantize_dz2(s):
+            quantize(dz2_mx[s], E5M2, dz2_t[s], "p j g b t -> p (j g b t)")
 
-        def make_dh(u, j):
-            h, s = divmod(u, 8)
-            bank = psum.tile([P, KP], F32, name="dh", bufs=3)
-            for g in range(2):
-                mx(bank, dz2_q[s], P * (2 * j + g), E5, w2_q[(h, g)], E4, g == 0, g == 1)
-            dh[(u, j)] = bank
+        sign1, dh, dp, db_sum, db, da_bank = {}, {}, {}, {}, {}, {}
 
-        def mask1(u, engine):
-            tile = work.tile([P, 2, 4, P], BF16, name="sign1", bufs=S1_BUFS)
-            sign_of(engine, tile[:].rearrange("b j t p -> b j p t"), raw[("z1", u)][:].rearrange("b j (p t) -> b j p t", t=4))
-            sign1[u] = tile
-            release(("z1", u))
+        def make_dh(step, j):
+            h, s = divmod(step, STEPS)
+            dh[(step, j)] = new_bank("dh", [P, KP])
+            for g in two:
+                mx_pass(dh[(step, j)], dz2_mx[s], P * (2 * j + g), E5M2, w2_mx[(h, g)], E4M3, g == 0, g == 1)
 
-        def make_dp(u, j):
-            h, s = divmod(u, 8)
-            i, node = s // 2, 2 * (s % 2) + j
-            tile = work.tile([P, KP], F32, name="dp", bufs=DP_BUFS)
-            nc.vector.scalar_tensor_tensor(out=tile[:], in0=sign1[u][:, j].rearrange("b t p -> b (t p)"), scalar=SLOPE, in1=dh[(u, j)][:],
-                                           op0=ALU.max, op1=ALU.mult)
-            dp[(h, i, node)] = tile
-            if u < 15:
-                add_db(u, j, nc.gpsimd)
+        def make_sign1(step, engine):
+            sign1[step] = work.tile([P, 2, 4, P], BF16, name="sign1", bufs=3)
+            sign_on(engine, sign1[step][:].rearrange("b j t p -> b j p t"),
+                    loaded[("z1", step)][:].rearrange("b j (p t) -> b j p t", t=4))
+            release(("z1", step))
 
-        def add_db(u, j, adder):
-            h, s = divmod(u, 8)
-            i, node = s // 2, 2 * (s % 2) + j
-            tile = dp[(h, i, node)]
+        def pair_of(step, j):
+            h, s = divmod(step, STEPS)
+            return h, s // 2, 2 * (s % 2) + j
+
+        def make_dp(step, j):
+            pair = pair_of(step, j)
+            dp[pair] = work.tile([P, KP], F32, name="dp", bufs=DP_BUFS)
+            nc.vector.scalar_tensor_tensor(out=dp[pair][:], in0=sign1[step][:, j].rearrange("b t p -> b (t p)"), scalar=SLOPE,
+                                           in1=dh[(step, j)][:], op0=ALU.max, op1=ALU.mult)
+
+        def add_to_db(step, j, engine):
+            h, i, node = pair_of(step, j)
             if i == 1:
-                acc[node] = work.tile([P, KP], F32, name="acc", bufs=4)
-                adder.tensor_tensor(out=acc[node][:], in0=dp[(h, 0, node)][:], in1=tile[:], op=ALU.add)
-            elif i == 2:
-                adder.tensor_tensor(out=acc[node][:], in0=acc[node][:], in1=tile[:], op=ALU.add)
-            elif i == 3:
-                if node == 0:
-                    db[h] = work.tile([P, NODES, KP], BF16, name="db", bufs=1)
-                adder.tensor_tensor(out=db[h][:, node], in0=acc[node][:], in1=tile[:], op=ALU.add)
+                db_sum[node] = work.tile([P, KP], F32, name="db_sum", bufs=NODES)
+            if (i, node) == (NODES - 1, 0):
+                db[h] = work.tile([P, NODES, KP], BF16, name="db", bufs=1)
+            if i > 0:
+                engine.tensor_tensor(out=db[h][:, node] if i == NODES - 1 else db_sum[node][:],
+                                     in0=dp[(h, 0, node)][:] if i == 1 else db_sum[node][:], in1=dp[(h, i, node)][:], op=ALU.add)
 
-        def sum_da_pe(h, i):
-            bank = psum.tile([P, 4, P], F32, name="da", bufs=1)
+        def add_to_da(h, i, node, t, start, stop):
+            nc.tensor.matmul(da_bank[(h, i)][:, t, :], lhsT=dp[(h, i, node)][:, P * t:P * (t + 1)], rhs=ident32[:],
+                             start=start, stop=stop, is_transpose=True)
+
+        def sum_da(h, i):
+            da_bank[(h, i)] = new_bank("da", [P, 4, P])
             for t in range(4):
                 for node in range(NODES):
-                    nc.tensor.matmul(bank[:, t, :], lhsT=dp[(h, i, node)][:, P * t:P * (t + 1)], rhs=ident32[:],
-                                     start=node == 0, stop=node == NODES - 1, is_transpose=True)
-            return bank
+                    add_to_da(h, i, node, t, node == 0, node == NODES - 1)
 
-        def sum_da_node(h, i, node, bank):
-            for t in range(4):
-                nc.tensor.matmul(bank[:, t, :], lhsT=dp[(h, i, node)][:, P * t:P * (t + 1)], rhs=ident32[:],
-                                 start=(node, t) == (0, 0), stop=(node, t) == (NODES - 1, 3), is_transpose=True)
+        def sum_last_da(step):
+            for j in two:
+                h, i, node = pair_of(step, j)
+                if node == 0:
+                    da_bank[(h, i)] = new_bank("da", [P, 4, P])
+                for t in range(4):
+                    add_to_da(h, i, node, t, (node, t) == (0, 0), (node, t) == (NODES - 1, 3))
 
-        def sum_da_out(h, i, bank, engine):
+        dz1_feat, dz1_tok = {}, {}
+
+        def new_feat(a, h):
+            dz1_feat[(a, h)] = work.tile([P, NODES, P, 4], BF16, name="dz1_feat", bufs=3, align_bytes=64)
+
+        def new_tok(a, h):
+            dz1_tok[(a, h)] = work.tile([P, KP, NODES], BF16, name="dz1_tok", bufs=2, align_bytes=64)
+
+        def round_da(h, i):
             if i == 0:
-                feat[(0, h)] = work.tile([P, NODES, P, 4], BF16, name="feat", bufs=3, align_bytes=64)
-            copy_on(engine, feat[(0, h)][:, i], bank[:].rearrange("p t b -> p b t"))
+                new_feat(0, h)
+            nc.scalar.copy(out=dz1_feat[(0, h)][:, i], in_=da_bank[(h, i)][:].rearrange("p t b -> p b t"))
 
-        def quant_feat(a, h):
-            quantize(feat_q[(a, h)], 0, E5, feat[(a, h)][:].rearrange("p n b t -> p (n b t)"))
-
-        def back_a_pe(h, u, tag):
-            words = feat[(0, h)][:].rearrange("p n b t -> p (n b t)").bitcast(F32)
-            bank = psum.tile([P, NODES, P], F32, name=tag, bufs=2)
+        def turn_da(h, u, role):
+            words = dz1_feat[(0, h)][:].rearrange("p n b t -> p (n b t)").bitcast(F32)
+            bank = new_bank(role, [P, NODES, P])
             for i in range(NODES):
                 nc.tensor.transpose(bank[:, i, :], words[:, 256 * i + u:256 * (i + 1):2], ident32[:])
             return bank
 
-        def back_a_out(h, u, bank, engine):
+        def copy_da_tok(h, u, bank, engine):
             if u == 0:
-                tok[(0, h)] = work.tile([P, KP, NODES], BF16, name="tok", bufs=2, align_bytes=64)
+                new_tok(0, h)
             values = bank[:].rearrange("b n p -> b (n p)").bitcast(BF16).rearrange("b (n c) -> b c n", n=NODES)
-            copy_on(engine, tok[(0, h)][:, 256 * u:256 * (u + 1), :], values)
+            copy_on(engine, dz1_tok[(0, h)][:, 256 * u:256 * (u + 1), :], values)
 
-        def weave(engine, out, in_):
-            if engine == "G":
-                nc.gpsimd.tensor_scalar(out=out, in0=in_.rearrange("b n c -> b c n"), scalar1=1.0, scalar2=0.0, op0=ALU.mult, op1=ALU.add)
-            else:
-                copy_on(engine, out.rearrange("b (c i) n -> b c n i", i=4), in_.rearrange("b n (c i) -> b c n i", i=4))
+        def interleave_db(h, engine, first, last):
+            if first == 0:
+                new_tok(1, h)
+            copy_on(engine, dz1_tok[(1, h)][:, first:last, :].rearrange("b (c i) n -> b c n i", i=4),
+                    db[h][:, :, first:last].rearrange("b n (c i) -> b c n i", i=4))
 
-        def tok_b(h, engines):
-            tok[(1, h)] = work.tile([P, KP, NODES], BF16, name="tok", bufs=2, align_bytes=64)
-            for engine, c0, c1 in engines:
-                weave(engine, tok[(1, h)][:, c0:c1, :], db[h][:, :, c0:c1])
-
-        def quant_tok(a, h):
-            quantize(tok_q[(a, h)], 0, E5, tok[(a, h)][:].rearrange("b c n -> b (c n)"))
-
-        def feat_b_pe(h, q, tag):
-            bank = psum.tile([P, 2, 4, P], BF16, name=tag, bufs=2)
-            for r in range(2):
+        def turn_db(h, q, role):
+            bank = new_bank(role, [P, 2, 4, P], BF16)
+            for r in two:
                 for t in range(4):
                     nc.tensor.transpose(bank[:, r, t, :], db[h][:, 2 * q + r, P * t:P * (t + 1)], ident16[:])
             return bank
 
-        def feat_b_out(h, q, bank, engine):
+        def copy_db_feat(h, q, bank):
             if q == 0:
-                feat[(1, h)] = work.tile([P, NODES, P, 4], BF16, name="feat", bufs=3, align_bytes=64)
-            copy_on(engine, feat[(1, h)][:, 2 * q:2 * q + 2], bank[:].rearrange("p r t b -> p r b t"))
+                new_feat(1, h)
+            nc.vector.tensor_copy(out=dz1_feat[(1, h)][:, 2 * q:2 * q + 2], in_=bank[:].rearrange("p r t b -> p r b t"))
 
-        def weave_f(x, engine):
-            tile = work.tile([P, KP, NODES], BF16, name="dz2t", bufs=2, align_bytes=64)
-            weave(engine, tile[:], raw[("f", x)][:])
-            release(("f", x))
+        def quantize_feat(a, h):
+            quantize(dz1_feat_mx[(a, h)], E5M2, dz1_feat[(a, h)], "p n b t -> p (n b t)")
+
+        def quantize_tok(a, h):
+            quantize(dz1_tok_mx[(a, h)], E5M2, dz1_tok[(a, h)], "b c n -> b (c n)")
+
+        def interleave_f(x):
+            tile = work.tile([P, KP, NODES], BF16, name="dz2_t", bufs=2, align_bytes=64)
+            nc.gpsimd.tensor_scalar(out=tile[:], in0=loaded[("f", 0)][:, :, KP * x:KP * (x + 1)].rearrange("b n c -> b c n"),
+                                    scalar1=1.0, scalar2=0.0, op0=ALU.mult, op1=ALU.add)
+            if x == 1:
+                release(("f", 0))
             return tile
 
-        def out1_pe(a, h, m, tag, bufs):
-            bank = psum.tile([P, KP], F32, name=tag, bufs=bufs)
-            mx(bank, f_q[m // 4], P * (m % 4), E4, tok_q[(a, h)], E5, True, True)
+        staged = {}
+
+        def stage_for(key, part):
+            if part == 0:
+                staged[key] = work.tile([P, 2, KP], F32, name="small", bufs=SMALL_BUFS)
+            return staged[key]
+
+        def multiply_out1(a, h, m, role):
+            bank = new_bank(role, [P, KP])
+            mx_pass(bank, f_mx[m // 4], P * (m % 4), E4M3, dz1_tok_mx[(a, h)], E5M2, True, True)
             return bank
 
-        def out1_out(a, h, m, bank, engine):
-            stage = work.tile([P, KP], F32, name="raw", bufs=RAW_BUFS)
+        def store_out1(a, h, m, bank, engine):
+            stage = stage_for((a, h, m // 2), m % 2)
             if a == 0:
-                copy_on(engine, stage[:].rearrange("c (p u e) -> c p u e", u=2, e=2), bank[:].rearrange("c (u p e) -> c p u e", u=2, e=2))
+                copy_on(engine, stage[:, m % 2].rearrange("c (p u e) -> c p u e", u=2, e=2),
+                        bank[:].rearrange("c (u p e) -> c p u e", u=2, e=2))
             else:
-                copy_on(engine, stage[:].rearrange("c (p t) -> c p t", t=4), bank[:].rearrange("c (t p) -> c p t", t=4))
-            nc.sync.dma_start(out=out_1[C * a + P * m:C * a + P * (m + 1), KP * h:KP * (h + 1)], in_=stage[:])
+                copy_on(engine, stage[:, m % 2].rearrange("c (p t) -> c p t", t=4), bank[:].rearrange("c (t p) -> c p t", t=4))
+            if m % 2 == 1:
+                rows = out_1[C * a + P * (m - 1):C * a + P * (m + 1), KP * h:KP * (h + 1)]
+                nc.sync.dma_start(out=rows.rearrange("(r c) k -> c r k", r=2), in_=stage[:])
 
-        def out0_pe(n, x, h, bank):
-            for a in range(2):
-                mx(bank, feat_q[(a, h)], P * n, E5, w1_q[(a, x, h)], E4, (h, a) == (0, 0), (h, a) == (1, 1))
+        def multiply_out0(node, x, h, bank):
+            for a in two:
+                mx_pass(bank, dz1_feat_mx[(a, h)], P * node, E5M2, w1_mx[(a, x, h)], E4M3, (h, a) == (0, 0), (h, a) == (1, 1))
 
-        def out0_out(n, x, bank, engine):
-            stage = work.tile([P, KP], F32, name="raw", bufs=RAW_BUFS)
-            copy_on(engine, stage[:].rearrange("b (m r) -> b m r", r=4), bank[:].rearrange("b (r m) -> b m r", r=4))
-            nc.sync.dma_start(out=out_0[:, n, KP * x:KP * (x + 1)], in_=stage[:])
+        def store_out0(node, x, bank, engine):
+            stage = stage_for(node, x)
+            copy_on(engine, stage[:, x].rearrange("b (m r) -> b m r", r=4), bank[:].rearrange("b (r m) -> b m r", r=4))
+            if node == NODES - 1:
+                nc.sync.dma_start(out=out_0[:, node, KP * x:KP * (x + 1)], in_=stage[:, x])
+            elif x == 1:
+                nc.sync.dma_start(out=out_0[:, node, :], in_=stage[:].rearrange("b x c -> b (x c)"))
 
-        pump()
-        mask2(0, 0, "S")
-        for g in range(2):
-            bank = turn_pe(("g", 0), g)
-            turn_out(("g", 0), g, bank, "S")
-        mask2(0, 1, "V")
-        turn2(0, 0)
-        turn2(0, 1)
+        issue_loads()
+        make_sign2(0, 0, "scalar")
+        run_turns([(("grad", 0), 0, g) for g in two], ["turn"])
+        make_sign2(0, 1, "vector")
+        turn_sign2(0, 0)
+        turn_sign2(0, 1)
 
-        pending = []
-        late = []
-        f_woven = {}
-        out1_left = [(a, 0, m) for a in (1, 0) for m in range(8)]
-        spare = ["tz", "misc"]
-        count = 0
-
-        def run_jobs(some, tags, engines):
-            for k, (unit, g) in enumerate(some):
-                turn_out(unit, g, turn_pe(unit, g, tags[k % len(tags)]), engines[k % len(engines)])
-            return [(unit, g) for unit, g in some if unit[0] != "g" and unit[2] == 1]
-
-        for tick in range(18):
-            u_p = tick - 2
-            u_x = tick - 1
-            first = tick < 8
-            tick_jobs = [job for job in jobs if job_tick[job] == tick]
-            staged = []
+        last_step = 2 * STEPS - 1
+        spare_roles = ["signs", "turn"]
+        out1_tiles = [(a, 0, m) for a in (1, 0) for m in range(8)]
+        spare_used = 0
+        to_quantize = []
+        for tick in range(2 * STEPS + 2):
+            dp_step, dh_step = tick - 2, tick - 1
+            makes_dz2 = tick < STEPS and tick != 1
+            next_signs = tick + 1 < STEPS
+            has_dh = 0 <= dh_step <= last_step
+            turns = [t for t in later_turns if turn_tick[t] == tick]
+            roles = ["turn"] if tick < STEPS else spare_roles
+            sign1_engine = "vector" if tick == 1 or (next_signs and len(turns) == 4) else "scalar"
             if tick == 1:
                 make_dz2(1, 0, 0)
                 make_dz2(1, 0, 1)
-                staged = run_jobs(tick_jobs, ["misc"], "S")
-                make_dz2(1, 1, 0)
-                turn_quant(*staged[0])
-                make_dz2(1, 1, 1)
-                turn_quant(*staged[1])
-                staged = []
-                tick_jobs = []
-            if tick + 1 < 8:
-                mask2(tick + 1, 0, "S")
-            if 0 <= u_x < 16 and u_x not in M1_V:
-                mask1(u_x, "S")
-            if u_p >= 0:
-                make_dp(u_p, 0)
-            if 0 <= u_x < 16:
-                make_dh(u_x, 0)
-            held = []
-            if tick >= 11:
-                for k in range(OUTS[tick - 11]):
-                    job = out1_left[0]
-                    out1_left.remove(job)
-                    held.append((job, out1_pe(*job, spare[count % 2], 2)))
-                    count = count + 1
-            if first and tick != 1:
+                whole = run_turns(turns_of(weight_blocks[0]), roles)
+                for j in two:
+                    make_dz2(1, 1, j)
+                    quantize_weight(*whole[j])
+            if next_signs:
+                make_sign2(tick + 1, 0, "scalar")
+            if has_dh and sign1_engine == "scalar":
+                make_sign1(dh_step, "scalar")
+            if dp_step >= 0:
+                make_dp(dp_step, 0)
+                if dp_step < last_step:
+                    add_to_db(dp_step, 0, nc.gpsimd)
+            if has_dh:
+                make_dh(dh_step, 0)
+            tiles = out1_tiles[:3 - tick % 2] if tick > STEPS + 2 else []
+            out1_tiles = out1_tiles[len(tiles):]
+            banks = [multiply_out1(*tile, spare_roles[(spare_used + k) % 2]) for k, tile in enumerate(tiles)]
+            spare_used = spare_used + len(tiles)
+            if makes_dz2:
                 make_dz2(tick, 0, 0)
-            if tick - F_AT in (0, 1):
-                f_woven[tick - F_AT] = weave_f(tick - F_AT, F_ENG)
-            if u_p >= 0:
-                make_dp(u_p, 1)
-            if first and tick != 1:
+            if tick in (2, 3):
+                f_tile = interleave_f(tick - 2)
+            if dp_step >= 0:
+                make_dp(dp_step, 1)
+                if dp_step < last_step:
+                    add_to_db(dp_step, 1, nc.gpsimd)
+            if makes_dz2:
                 make_dz2(tick, 0, 1)
-            if tick + 1 < 8 and tick + 1 not in M2_V and not EVAC_FIRST:
-                mask2(tick + 1, 1, "S")
-            for k, (job, bank) in enumerate(held):
-                out1_out(*job, bank, "V" if k < OUT_V and tick < 17 else "S")
-            if tick == 10:
-                turned = [back_a_pe(0, u, "tz") for u in range(2)]
-                tok_b(0, [(TB_ENG, 0, KP)])
-                for u in range(2):
-                    back_a_out(0, u, turned[u], "S")
-                quant_tok(1, 0)
-            if tick == 11:
-                quant_tok(0, 0)
-                quant_feat(0, 0)
-            staged.extend(run_jobs(tick_jobs[:2], ["misc"] if first else spare, "S" if first else EV8))
-            if tick + 1 < 8 and tick + 1 not in M2_V and EVAC_FIRST:
-                mask2(tick + 1, 1, "S")
-            if tick + 1 < 8:
-                turn2(tick + 1, 0)
-            if 0 <= u_x < 16:
-                make_dh(u_x, 1)
-            if first and tick != 1:
+            if next_signs and tick > 0:
+                make_sign2(tick + 1, 1, "scalar")
+            for k, tile in enumerate(tiles):
+                store_out1(*tile, banks[k], "vector" if k == 0 and dp_step < last_step else "scalar")
+            if tick == STEPS + 2:
+                da_turned = [turn_da(0, u, "signs") for u in two]
+                interleave_db(0, "vector", 0, KP)
+                for u in two:
+                    copy_da_tok(0, u, da_turned[u], "scalar")
+                quantize_tok(1, 0)
+            if tick == STEPS + 3:
+                quantize_tok(0, 0)
+                quantize_feat(0, 0)
+            whole = run_turns(turns[:2], roles)
+            if next_signs:
+                turn_sign2(tick + 1, 0)
+            if has_dh:
+                make_dh(dh_step, 1)
+            if makes_dz2:
                 make_dz2(tick, 1, 0)
                 make_dz2(tick, 1, 1)
-            if tick + 1 < 8 and tick + 1 in M2_V:
-                mask2(tick + 1, 1, "V")
-            for job in pending:
-                if job[0][0] == "w1" and job[0][1] >= W1_LATE:
-                    late.append(job)
-                else:
-                    turn_quant(*job)
-            if tick >= 8:
-                for job in late[:LATE_N]:
-                    turn_quant(*job)
-                late = late[LATE_N:]
-            if 0 <= u_x < 16 and u_x in M1_V:
-                mask1(u_x, "V")
-            if tick + 1 < 8 and T2_FIRST:
-                turn2(tick + 1, 1)
-            staged.extend(run_jobs(tick_jobs[2:], ["misc"] if first else spare, "S"))
-            pending = staged
-            if tick - FB_AT in (0, 2):
-                q = (tick - FB_AT) // 2
-                feat_b_out(0, q, feat_b_pe(0, q, spare[count % 2]), FB_ENG[q])
-                count = count + 1
-            if u_p >= 0 and u_p % 2 == 1 and u_p < 15:
-                h, i = u_p // 8, (u_p % 8) // 2
-                bank = sum_da_pe(h, i)
-                sum_da_out(h, i, bank, "S")
-            if u_p == 14:
-                last_bank = psum.tile([P, 4, P], F32, name="da", bufs=1)
-            if u_p >= 14:
-                for j in range(2):
-                    sum_da_node(1, 3, 2 * (u_p % 2) + j, last_bank)
-            if tick + 1 < 8 and not T2_FIRST:
-                turn2(tick + 1, 1)
-            if first:
-                quant_dz2(tick)
-            if tick - F_AT in (0, 1):
-                quantize(f_q[tick - F_AT], 0, E4, f_woven[tick - F_AT][:].rearrange("b c n -> b (c n)"))
+            if tick == 0:
+                make_sign2(1, 1, "vector")
+            for operand in to_quantize:
+                quantize_weight(*operand)
+            if has_dh and sign1_engine == "vector":
+                make_sign1(dh_step, "vector")
+            to_quantize = whole + run_turns(turns[2:], roles)
+            if tick in (DB_TURN_TICK, DB_TURN_TICK + 2):
+                q = (tick - DB_TURN_TICK) // 2
+                copy_db_feat(0, q, turn_db(0, q, spare_roles[spare_used % 2]))
+                spare_used = spare_used + 1
+            if dp_step >= last_step - 1:
+                sum_last_da(dp_step)
+            elif dp_step % 2 == 1 and dp_step > 0:
+                h, i, node = pair_of(dp_step, 1)
+                sum_da(h, i)
+                round_da(h, i)
+            if next_signs:
+                turn_sign2(tick + 1, 1)
+            if tick < STEPS:
+                quantize_dz2(tick)
+            if tick in (2, 3):
+                quantize(f_mx[tick - 2], E4M3, f_tile, "b c n -> b (c n)")
 
-        for j in range(2):
-            add_db(15, j, nc.vector)
-        sum_da_out(1, 3, last_bank, "S")
-        tok_b(1, [("S", 0, TB_SPLIT), ("V", TB_SPLIT, KP)])
-        quant_tok(1, 1)
-        a_banks = [back_a_pe(1, u, spare[(count + u) % 2]) for u in range(2)]
-        b_banks = [feat_b_pe(1, q, spare[(count + q) % 2]) for q in range(2)]
-        for u in range(2):
-            back_a_out(1, u, a_banks[u], "SV"[u])
-        tiles1 = [(a, 1, m) for a in (1, 0) for m in range(8)]
-        tiles0 = [(n, x) for x in range(2) for n in range(NODES)]
-        ring = [("dh", 3), ("dh", 3), ("dh", 3), ("da", 1)]
-        late = sorted(late, key=lambda job: (job[1], job[0][1] % 2))
-        chain = [lambda: quant_tok(0, 1), lambda: feat_b_out(1, 0, b_banks[0], "V"), lambda: feat_b_out(1, 1, b_banks[1], "V"), lambda: quant_feat(1, 0)]
-        chain.extend([lambda job=job: turn_quant(*job) for job in late if job[1] == 0])
-        n_first = len(chain)
-        chain.extend([lambda: quant_feat(0, 1), lambda: quant_feat(1, 1)])
-        chain.extend([lambda job=job: turn_quant(*job) for job in late if job[1] == 1])
-        for step in chain[:n_first]:
-            step()
-        opened = {}
-        for k, job in enumerate(tiles1):
-            bank = out1_pe(*job, *ring[k % 4])
-            if k == 8:
-                for step in chain[n_first:]:
-                    step()
-            out1_out(*job, bank, "S" if k < S_ONLY or k % 2 == 1 else "V")
-            if k >= OPEN_AT and (k - OPEN_AT) % 2 == 0 and len(opened) < 4:
-                n, x = tiles0[len(opened)]
-                opened[(n, x)] = psum.tile([P, KP], F32, name=spare[(count + len(opened)) % 2], bufs=2)
-                out0_pe(n, x, 0, opened[(n, x)])
-        for k, (n, x) in enumerate(tiles0):
-            if (n, x) not in opened:
-                tag, bufs = ring[k % 4]
-                opened[(n, x)] = psum.tile([P, KP], F32, name=tag, bufs=bufs)
-                out0_pe(n, x, 0, opened[(n, x)])
-            out0_pe(n, x, 1, opened[(n, x)])
-            out0_out(n, x, opened[(n, x)], "VS"[k % 2])
+        for j in two:
+            add_to_db(last_step, j, nc.vector)
+        round_da(1, NODES - 1)
+        interleave_db(1, "scalar", 0, SCALAR_COLUMNS)
+        interleave_db(1, "vector", SCALAR_COLUMNS, KP)
+        quantize_tok(1, 1)
+        quantize_feat(1, 0)
+        da_turned = [turn_da(1, u, spare_roles[(spare_used + u) % 2]) for u in two]
+        db_turned = [turn_db(1, q, spare_roles[(spare_used + q) % 2]) for q in two]
+        out_roles = ["dh", "dh", "dh", "da"]
+        out0_tiles = [(node, x) for node in range(NODES) for x in two]
+        out0_banks = {}
+        for k, tile in enumerate([(a, 1, m) for a in (1, 0) for m in range(8)]):
+            bank = multiply_out1(*tile, out_roles[k % 4])
+            if k == 1:
+                copy_da_tok(1, 0, da_turned[0], "vector")
+            store_out1(*tile, bank, "scalar")
+            if k == 1:
+                copy_da_tok(1, 1, da_turned[1], "vector")
+                quantize_tok(0, 1)
+                for q in two:
+                    copy_db_feat(1, q, db_turned[q])
+                quantize_feat(0, 1)
+                quantize_feat(1, 1)
+            if k >= OPEN_AFTER and k % 2 == 0 and len(out0_banks) < 4:
+                node, x = out0_tiles[len(out0_banks)]
+                out0_banks[(node, x)] = new_bank(spare_roles[(spare_used + len(out0_banks)) % 2], [P, KP])
+                multiply_out0(node, x, 0, out0_banks[(node, x)])
+        for k, (node, x) in enumerate(out0_tiles):
+            if (node, x) not in out0_banks:
+                out0_banks[(node, x)] = new_bank(out_roles[k % 4], [P, KP])
+                multiply_out0(node, x, 0, out0_banks[(node, x)])
+            multiply_out0(node, x, 1, out0_banks[(node, x)])
+            store_out0(node, x, out0_banks[(node, x)], "vector" if x == 0 else "scalar")

from contextlib import ExitStack

import concourse.mybir as mybir
from concourse.masks import make_identity

F32 = mybir.dt.float32
BF16 = mybir.dt.bfloat16
U32 = mybir.dt.uint32
U8 = mybir.dt.uint8
E4M3 = mybir.dt.float8_e4m3fn_x4
E5M2 = mybir.dt.float8_e5m2_x4
ALU = mybir.AluOpType
ACT = mybir.ActivationFunctionType

P = 128
NODES = 4
C = 1024
KP = 512
STEPS = 8
SLOPE = 0.2
TINY = 2.0 ** -126
FLOPS = 2 * P * NODES * NODES * C * C + 2 * (2 * P * NODES * 2 * C * C)
BYTES = 2 * (2 * P * NODES * C + 3 * C * C) + 4 * (2 * P * NODES * NODES * C + P * NODES * C + 2 * C * C)

BIG_BUFS = 5
SMALL_BUFS = 8
DP_BUFS = 9
SCALAR_COLUMNS = 176
DB_TURN_TICK = 13
OPEN_AFTER = 6


def tile_nonlocalmp_pa_v_kernel(tc, F, W1, b1, W2, b2, z1, z2, grad_out, out_0, out_1):
    nc = tc.nc
    with ExitStack() as ctx:
        keep = ctx.enter_context(tc.tile_pool(name="keep", bufs=1))
        work = ctx.enter_context(tc.tile_pool(name="work", bufs=2))
        psum = ctx.enter_context(tc.psum_pool(name="psum", bufs=1))
        ctx.enter_context(tc.manual_schedule())

        ident32 = keep.tile([P, P], F32, name="ident32")
        ident16 = keep.tile([P, P], BF16, name="ident16")
        make_identity(nc, ident32[:])
        make_identity(nc, ident16[:])

        bank_count = {"dh": 3, "signs": 2, "turn": 2, "da": 1}

        def new_bank(role, shape, dtype=F32):
            return psum.tile(shape, dtype, name=role, bufs=bank_count[role])

        def mx_operand(name):
            codes = keep.tile([P, KP], U32, name=name + "_codes", align_bytes=64)
            scales = keep.tile([P, KP], U8, name=name + "_scales", align_bytes=64)
            return codes, scales

        two = range(2)
        dz2_mx = [mx_operand("dz2_%d" % s) for s in range(STEPS)]
        w2_mx = {(h, g): mx_operand("w2_%d%d" % (h, g)) for h in two for g in two}
        w1_mx = {(a, x, h): mx_operand("w1_%d%d%d" % (a, x, h)) for a in two for x in two for h in two}
        f_mx = [mx_operand("f_%d" % x) for x in two]
        dz1_feat_mx = {(a, h): mx_operand("dz1f_%d%d" % (a, h)) for a in two for h in two}
        dz1_tok_mx = {(a, h): mx_operand("dz1t_%d%d" % (a, h)) for a in two for h in two}
        grad_t = {(g, q): keep.tile([P, 2, P, 4], BF16, name="grad_t%d%d" % (g, q)) for g in two for q in two}

        def quantize(operand, fmt, tile, pattern):
            nc.vector.quantize_mx(out=operand[0][:].bitcast(fmt), scales=operand[1][:], in_=tile[:].rearrange(pattern))

        def mx_pass(bank, lhs, column, lhs_fmt, rhs, rhs_fmt, start, stop):
            cols = slice(column, column + P)
            nc.tensor.matmul_mx(out=bank[:], lhsT=lhs[0][:, cols].bitcast(lhs_fmt), lhsT_scale=lhs[1][:, cols],
                                rhs=rhs[0][:].bitcast(rhs_fmt), rhs_scale=rhs[1][:], start=start, stop=stop)

        def copy_on(engine, out, in_):
            if engine == "scalar":
                nc.scalar.copy(out=out, in_=in_)
            else:
                nc.vector.tensor_copy(out=out, in_=in_)

        weight_blocks = [("w2", 0), ("w2", 1)] + [("w1", x) for x in range(4)]

        def turns_of(block):
            return [(block, q, g) for g in two for q in two]

        later_turns = [(("grad", 1), 0, g) for g in two] + [turn for block in weight_blocks[1:] for turn in turns_of(block)]
        later_ticks = [t for t in range(3, 10) for k in range(2 if t % 2 == 1 and t < 9 else 4)]
        turn_tick = dict(zip(turns_of(weight_blocks[0]) + later_turns, [1] * 4 + later_ticks))

        def source(key):
            kind, n = key
            if kind == "z2_first":
                return z2[:, 0, 0:2, KP * n:KP * (n + 1)]
            if kind == "z2":
                return z2[:, n // 2, 2 * (n % 2):2 * (n % 2) + 2, :]
            if kind == "z1":
                h, s = divmod(n, STEPS)
                return z1[:, s // 2, 2 * (s % 2):2 * (s % 2) + 2, KP * h:KP * (h + 1)]
            if kind == "grad":
                return grad_out[:, 2 * n:2 * n + 2, :]
            if kind == "f":
                return F
            return (W2 if kind == "w2" else W1)[KP * n:KP * (n + 1), :].rearrange("(m r) k -> m r k", r=4)

        load_order = [("z2_first", 0), ("grad", 0), ("z2_first", 1)]
        for tick in range(1, 2 * STEPS + 1):
            load_order.extend([("z2", tick)] if tick == 1 else [])
            load_order.extend([block for block in weight_blocks if turn_tick[(block, 0, 0)] == tick])
            load_order.extend([("z2", tick + 1)] if tick + 1 < STEPS else [])
            load_order.append(("z1", tick - 1))
            load_order.extend({1: [("f", 0)], 2: [("grad", 1)]}.get(tick, []))
        depth = {"big": BIG_BUFS, "small": SMALL_BUFS}
        size = {key: "small" if key[0] in ("z2_first", "z1", "grad") else "big" for key in load_order}
        loaded = {}
        used_up = set()

        def issue_loads():
            for key in load_order[len(loaded):]:
                earlier = [other for other in loaded if size[other] == size[key]]
                if len(earlier) >= depth[size[key]] and earlier[len(earlier) - depth[size[key]]] not in used_up:
                    return
                src = source(key)
                loaded[key] = work.tile(list(src.shape), src.dtype, name=size[key], bufs=depth[size[key]])
                nc.sync.dma_start(out=loaded[key][:], in_=src)

        def release(key):
            used_up.add(key)
            issue_loads()

        turned = {}

        def turn(block, q, g, role):
            is_grad = block[0] == "grad"
            words = loaded[block][:].rearrange("p r k -> p (r k)").bitcast(F32)
            bank = new_bank(role, [P, 2, 2, P])
            for r in two:
                first = KP * (2 * q + r) + 256 * g
                for u in two:
                    nc.tensor.transpose(bank[:, r, u, :], words[:, first + u:first + 256:2], ident32[:])
            if g == 1 and (is_grad or q == 1):
                release(block)
            if is_grad:
                dst = grad_t[(g, block[1])][:]
            else:
                if q == 0:
                    turned[(block, g)] = work.tile([P, 4, P, 4], BF16, name="turned", bufs=3, align_bytes=64)
                dst = turned[(block, g)][:, 2 * q:2 * q + 2]
            dst = dst.rearrange("p r m t -> p (r m t)").bitcast(F32).rearrange("p (r m u) -> p r m u", r=2, u=2)
            nc.scalar.copy(out=dst, in_=bank[:].rearrange("p r u m -> p r m u"))

        def run_turns(turns, roles):
            for k, (block, q, g) in enumerate(turns):
                turn(block, q, g, roles[k % len(roles)])
            return [(block, g) for block, q, g in turns if block[0] != "grad" and q == 1]

        def quantize_weight(block, g):
            kind, n = block
            operand = w2_mx[(n, g)] if kind == "w2" else w1_mx[(n // 2, n % 2, g)]
            quantize(operand, E4M3, turned[(block, g)], "p r m t -> p (r m t)")

        def sign_on(engine, out, in_):
            if engine == "scalar":
                nc.scalar.activation(out=out, in_=in_, func=ACT.Sign, bias=TINY)
            else:
                nc.vector.tensor_scalar(out=out, in0=in_, scalar1=0.0, scalar2=None, op0=ALU.is_ge)

        sign2, sign2_t, dz2_t = {}, {}, {}

        def make_sign2(s, g, engine):
            key = ("z2_first", g) if s == 0 else ("z2", s)
            z = loaded[key][:] if s == 0 else loaded[key][:, :, KP * g:KP * (g + 1)]
            sign2[(s, g)] = work.tile([P, 4, P, 2], BF16, name="sign2", bufs=3)
            sign_on(engine, sign2[(s, g)][:].rearrange("b t p j -> b p t j"), z.rearrange("b j (p t) -> b p t j", t=4))
            if s == 0 or g == 1:
                release(key)

        def turn_sign2(s, g):
            words = sign2[(s, g)][:].rearrange("b t p j -> b (t p j)").bitcast(F32)
            sign2_t[(s, g)] = new_bank("signs", [P, 4, P])
            for t in range(4):
                nc.tensor.transpose(sign2_t[(s, g)][:, t, :], words[:, P * t:P * (t + 1)], ident32[:])

        def make_dz2(s, g, j):
            if (g, j) == (0, 0):
                dz2_t[s] = work.tile([P, 2, 2, P, 4], BF16, name="dz2_t", bufs=2, align_bytes=64)
            signs = sign2_t[(s, g)][:].rearrange("p t b -> p (t b)").bitcast(BF16).rearrange("p (t b j) -> p j b t", t=4, j=2)
            i = s // 2
            nc.vector.scalar_tensor_tensor(out=dz2_t[s][:, j, g], in0=signs[:, j], scalar=SLOPE,
                                           in1=grad_t[(g, i // 2)][:, i % 2], op0=ALU.max, op1=ALU.mult)

        def quantize_dz2(s):
            quantize(dz2_mx[s], E5M2, dz2_t[s], "p j g b t -> p (j g b t)")

        sign1, dh, dp, db_sum, db, da_bank = {}, {}, {}, {}, {}, {}

        def make_dh(step, j):
            h, s = divmod(step, STEPS)
            dh[(step, j)] = new_bank("dh", [P, KP])
            for g in two:
                mx_pass(dh[(step, j)], dz2_mx[s], P * (2 * j + g), E5M2, w2_mx[(h, g)], E4M3, g == 0, g == 1)

        def make_sign1(step, engine):
            sign1[step] = work.tile([P, 2, 4, P], BF16, name="sign1", bufs=3)
            sign_on(engine, sign1[step][:].rearrange("b j t p -> b j p t"),
                    loaded[("z1", step)][:].rearrange("b j (p t) -> b j p t", t=4))
            release(("z1", step))

        def pair_of(step, j):
            h, s = divmod(step, STEPS)
            return h, s // 2, 2 * (s % 2) + j

        def make_dp(step, j):
            pair = pair_of(step, j)
            dp[pair] = work.tile([P, KP], F32, name="dp", bufs=DP_BUFS)
            nc.vector.scalar_tensor_tensor(out=dp[pair][:], in0=sign1[step][:, j].rearrange("b t p -> b (t p)"), scalar=SLOPE,
                                           in1=dh[(step, j)][:], op0=ALU.max, op1=ALU.mult)

        def add_to_db(step, j, engine):
            h, i, node = pair_of(step, j)
            if i == 1:
                db_sum[node] = work.tile([P, KP], F32, name="db_sum", bufs=NODES)
            if (i, node) == (NODES - 1, 0):
                db[h] = work.tile([P, NODES, KP], BF16, name="db", bufs=1)
            if i > 0:
                engine.tensor_tensor(out=db[h][:, node] if i == NODES - 1 else db_sum[node][:],
                                     in0=dp[(h, 0, node)][:] if i == 1 else db_sum[node][:], in1=dp[(h, i, node)][:], op=ALU.add)

        def add_to_da(h, i, node, t, start, stop):
            nc.tensor.matmul(da_bank[(h, i)][:, t, :], lhsT=dp[(h, i, node)][:, P * t:P * (t + 1)], rhs=ident32[:],
                             start=start, stop=stop, is_transpose=True)

        def sum_da(h, i):
            da_bank[(h, i)] = new_bank("da", [P, 4, P])
            for t in range(4):
                for node in range(NODES):
                    add_to_da(h, i, node, t, node == 0, node == NODES - 1)

        def sum_last_da(step):
            for j in two:
                h, i, node = pair_of(step, j)
                if node == 0:
                    da_bank[(h, i)] = new_bank("da", [P, 4, P])
                for t in range(4):
                    add_to_da(h, i, node, t, (node, t) == (0, 0), (node, t) == (NODES - 1, 3))

        dz1_feat, dz1_tok = {}, {}

        def new_feat(a, h):
            dz1_feat[(a, h)] = work.tile([P, NODES, P, 4], BF16, name="dz1_feat", bufs=3, align_bytes=64)

        def new_tok(a, h):
            dz1_tok[(a, h)] = work.tile([P, KP, NODES], BF16, name="dz1_tok", bufs=2, align_bytes=64)

        def round_da(h, i):
            if i == 0:
                new_feat(0, h)
            nc.scalar.copy(out=dz1_feat[(0, h)][:, i], in_=da_bank[(h, i)][:].rearrange("p t b -> p b t"))

        def turn_da(h, u, role):
            words = dz1_feat[(0, h)][:].rearrange("p n b t -> p (n b t)").bitcast(F32)
            bank = new_bank(role, [P, NODES, P])
            for i in range(NODES):
                nc.tensor.transpose(bank[:, i, :], words[:, 256 * i + u:256 * (i + 1):2], ident32[:])
            return bank

        def copy_da_tok(h, u, bank, engine):
            if u == 0:
                new_tok(0, h)
            values = bank[:].rearrange("b n p -> b (n p)").bitcast(BF16).rearrange("b (n c) -> b c n", n=NODES)
            copy_on(engine, dz1_tok[(0, h)][:, 256 * u:256 * (u + 1), :], values)

        def interleave_db(h, engine, first, last):
            if first == 0:
                new_tok(1, h)
            copy_on(engine, dz1_tok[(1, h)][:, first:last, :].rearrange("b (c i) n -> b c n i", i=4),
                    db[h][:, :, first:last].rearrange("b n (c i) -> b c n i", i=4))

        def turn_db(h, q, role):
            bank = new_bank(role, [P, 2, 4, P], BF16)
            for r in two:
                for t in range(4):
                    nc.tensor.transpose(bank[:, r, t, :], db[h][:, 2 * q + r, P * t:P * (t + 1)], ident16[:])
            return bank

        def copy_db_feat(h, q, bank):
            if q == 0:
                new_feat(1, h)
            nc.vector.tensor_copy(out=dz1_feat[(1, h)][:, 2 * q:2 * q + 2], in_=bank[:].rearrange("p r t b -> p r b t"))

        def quantize_feat(a, h):
            quantize(dz1_feat_mx[(a, h)], E5M2, dz1_feat[(a, h)], "p n b t -> p (n b t)")

        def quantize_tok(a, h):
            quantize(dz1_tok_mx[(a, h)], E5M2, dz1_tok[(a, h)], "b c n -> b (c n)")

        def interleave_f(x):
            tile = work.tile([P, KP, NODES], BF16, name="dz2_t", bufs=2, align_bytes=64)
            nc.gpsimd.tensor_scalar(out=tile[:], in0=loaded[("f", 0)][:, :, KP * x:KP * (x + 1)].rearrange("b n c -> b c n"),
                                    scalar1=1.0, scalar2=0.0, op0=ALU.mult, op1=ALU.add)
            if x == 1:
                release(("f", 0))
            return tile

        staged = {}

        def stage_for(key, part):
            if part == 0:
                staged[key] = work.tile([P, 2, KP], F32, name="small", bufs=SMALL_BUFS)
            return staged[key]

        def multiply_out1(a, h, m, role):
            bank = new_bank(role, [P, KP])
            mx_pass(bank, f_mx[m // 4], P * (m % 4), E4M3, dz1_tok_mx[(a, h)], E5M2, True, True)
            return bank

        def store_out1(a, h, m, bank, engine):
            stage = stage_for((a, h, m // 2), m % 2)
            if a == 0:
                copy_on(engine, stage[:, m % 2].rearrange("c (p u e) -> c p u e", u=2, e=2),
                        bank[:].rearrange("c (u p e) -> c p u e", u=2, e=2))
            else:
                copy_on(engine, stage[:, m % 2].rearrange("c (p t) -> c p t", t=4), bank[:].rearrange("c (t p) -> c p t", t=4))
            if m % 2 == 1:
                rows = out_1[C * a + P * (m - 1):C * a + P * (m + 1), KP * h:KP * (h + 1)]
                nc.sync.dma_start(out=rows.rearrange("(r c) k -> c r k", r=2), in_=stage[:])

        def multiply_out0(node, x, h, bank):
            for a in two:
                mx_pass(bank, dz1_feat_mx[(a, h)], P * node, E5M2, w1_mx[(a, x, h)], E4M3, (h, a) == (0, 0), (h, a) == (1, 1))

        def store_out0(node, x, bank, engine):
            stage = stage_for(node, x)
            copy_on(engine, stage[:, x].rearrange("b (m r) -> b m r", r=4), bank[:].rearrange("b (r m) -> b m r", r=4))
            if node == NODES - 1:
                nc.sync.dma_start(out=out_0[:, node, KP * x:KP * (x + 1)], in_=stage[:, x])
            elif x == 1:
                nc.sync.dma_start(out=out_0[:, node, :], in_=stage[:].rearrange("b x c -> b (x c)"))

        issue_loads()
        make_sign2(0, 0, "scalar")
        run_turns([(("grad", 0), 0, g) for g in two], ["turn"])
        make_sign2(0, 1, "vector")
        turn_sign2(0, 0)
        turn_sign2(0, 1)

        last_step = 2 * STEPS - 1
        spare_roles = ["signs", "turn"]
        out1_tiles = [(a, 0, m) for a in (1, 0) for m in range(8)]
        spare_used = 0
        to_quantize = []
        for tick in range(2 * STEPS + 2):
            dp_step, dh_step = tick - 2, tick - 1
            makes_dz2 = tick < STEPS and tick != 1
            next_signs = tick + 1 < STEPS
            has_dh = 0 <= dh_step <= last_step
            turns = [t for t in later_turns if turn_tick[t] == tick]
            roles = ["turn"] if tick < STEPS else spare_roles
            sign1_engine = "vector" if tick == 1 or (next_signs and len(turns) == 4) else "scalar"
            if tick == 1:
                make_dz2(1, 0, 0)
                make_dz2(1, 0, 1)
                whole = run_turns(turns_of(weight_blocks[0]), roles)
                for j in two:
                    make_dz2(1, 1, j)
                    quantize_weight(*whole[j])
            if next_signs:
                make_sign2(tick + 1, 0, "scalar")
            if has_dh and sign1_engine == "scalar":
                make_sign1(dh_step, "scalar")
            if dp_step >= 0:
                make_dp(dp_step, 0)
                if dp_step < last_step:
                    add_to_db(dp_step, 0, nc.gpsimd)
            if has_dh:
                make_dh(dh_step, 0)
            tiles = out1_tiles[:3 - tick % 2] if tick > STEPS + 2 else []
            out1_tiles = out1_tiles[len(tiles):]
            banks = [multiply_out1(*tile, spare_roles[(spare_used + k) % 2]) for k, tile in enumerate(tiles)]
            spare_used = spare_used + len(tiles)
            if makes_dz2:
                make_dz2(tick, 0, 0)
            if tick in (2, 3):
                f_tile = interleave_f(tick - 2)
            if dp_step >= 0:
                make_dp(dp_step, 1)
                if dp_step < last_step:
                    add_to_db(dp_step, 1, nc.gpsimd)
            if makes_dz2:
                make_dz2(tick, 0, 1)
            if next_signs and tick > 0:
                make_sign2(tick + 1, 1, "scalar")
            for k, tile in enumerate(tiles):
                store_out1(*tile, banks[k], "vector" if k == 0 and dp_step < last_step else "scalar")
            if tick == STEPS + 2:
                da_turned = [turn_da(0, u, "signs") for u in two]
                interleave_db(0, "vector", 0, KP)
                for u in two:
                    copy_da_tok(0, u, da_turned[u], "scalar")
                quantize_tok(1, 0)
            if tick == STEPS + 3:
                quantize_tok(0, 0)
                quantize_feat(0, 0)
            whole = run_turns(turns[:2], roles)
            if next_signs:
                turn_sign2(tick + 1, 0)
            if has_dh:
                make_dh(dh_step, 1)
            if makes_dz2:
                make_dz2(tick, 1, 0)
                make_dz2(tick, 1, 1)
            if tick == 0:
                make_sign2(1, 1, "vector")
            for operand in to_quantize:
                quantize_weight(*operand)
            if has_dh and sign1_engine == "vector":
                make_sign1(dh_step, "vector")
            to_quantize = whole + run_turns(turns[2:], roles)
            if tick in (DB_TURN_TICK, DB_TURN_TICK + 2):
                q = (tick - DB_TURN_TICK) // 2
                copy_db_feat(0, q, turn_db(0, q, spare_roles[spare_used % 2]))
                spare_used = spare_used + 1
            if dp_step >= last_step - 1:
                sum_last_da(dp_step)
            elif dp_step % 2 == 1 and dp_step > 0:
                h, i, node = pair_of(dp_step, 1)
                sum_da(h, i)
                round_da(h, i)
            if next_signs:
                turn_sign2(tick + 1, 1)
            if tick < STEPS:
                quantize_dz2(tick)
            if tick in (2, 3):
                quantize(f_mx[tick - 2], E4M3, f_tile, "b c n -> b (c n)")

        for j in two:
            add_to_db(last_step, j, nc.vector)
        round_da(1, NODES - 1)
        interleave_db(1, "scalar", 0, SCALAR_COLUMNS)
        interleave_db(1, "vector", SCALAR_COLUMNS, KP)
        quantize_tok(1, 1)
        quantize_feat(1, 0)
        da_turned = [turn_da(1, u, spare_roles[(spare_used + u) % 2]) for u in two]
        db_turned = [turn_db(1, q, spare_roles[(spare_used + q) % 2]) for q in two]
        out_roles = ["dh", "dh", "dh", "da"]
        out0_tiles = [(node, x) for node in range(NODES) for x in two]
        out0_banks = {}
        for k, tile in enumerate([(a, 1, m) for a in (1, 0) for m in range(8)]):
            bank = multiply_out1(*tile, out_roles[k % 4])
            if k == 1:
                copy_da_tok(1, 0, da_turned[0], "vector")
            store_out1(*tile, bank, "scalar")
            if k == 1:
                copy_da_tok(1, 1, da_turned[1], "vector")
                quantize_tok(0, 1)
                for q in two:
                    copy_db_feat(1, q, db_turned[q])
                quantize_feat(0, 1)
                quantize_feat(1, 1)
            if k >= OPEN_AFTER and k % 2 == 0 and len(out0_banks) < 4:
                node, x = out0_tiles[len(out0_banks)]
                out0_banks[(node, x)] = new_bank(spare_roles[(spare_used + len(out0_banks)) % 2], [P, KP])
                multiply_out0(node, x, 0, out0_banks[(node, x)])
        for k, (node, x) in enumerate(out0_tiles):
            if (node, x) not in out0_banks:
                out0_banks[(node, x)] = new_bank(out_roles[k % 4], [P, KP])
                multiply_out0(node, x, 0, out0_banks[(node, x)])
            multiply_out0(node, x, 1, out0_banks[(node, x)])
            store_out0(node, x, out0_banks[(node, x)], "vector" if x == 0 else "scalar")
